import numpy as np
import ml_dtypes


def mxq(x, axis, fmt="e4m3"):
    dtype, down = {"e4m3": (ml_dtypes.float8_e4m3fn, 7), "e5m2": (ml_dtypes.float8_e5m2, 14)}[fmt]
    v = np.moveaxis(np.asarray(x, np.float32).astype(ml_dtypes.bfloat16).astype(np.float64), axis, -1)
    blocks = v.reshape(v.shape[:-1] + (-1, 32))
    amax = np.abs(blocks).max(-1, keepdims=True)
    byte = np.maximum(np.where(amax > 0, np.frexp(amax)[1] - 1 + 127, 0) - down, 1)
    scale = np.exp2(byte - 127.0)
    codes = (blocks / scale).astype(np.float32).astype(dtype).astype(np.float64)
    return np.moveaxis((codes * scale).reshape(v.shape), -1, axis)


WIDE = False


def mx_kscale(k):
    if not WIDE:
        return np.ones(k)
    levels = np.array([10, -10, 5, -5, 0])
    if k % 512:
        return np.exp2(np.random.permutation(np.resize(levels, k // 32))).repeat(32)
    a = np.empty((k // 512, 16))
    for p in range(k // 512):
        a[p, :8] = np.random.permutation(np.resize(levels, 8))
        for g in range(8):
            far = levels[np.abs(levels - a[p, g]) >= 10]
            a[p, g + 8] = far[np.random.randint(len(far))]
    return np.exp2(a.ravel()).repeat(32)


BF16 = ml_dtypes.bfloat16


def bf(x):
    return np.asarray(x, np.float32).astype(BF16)


def f64(x):
    return np.asarray(x).astype(np.float64)


B, C, O, H, W, KH, KW, PAD = 4, 512, 512, 16, 16, 3, 3, 1
C_CURV = 0.01
EPS = 1e-7


def artanh(z):
    return 0.5 * np.log((1.0 + z) / (1.0 - z))


def log0(y):
    sqc = np.sqrt(C_CURV)
    n = np.maximum(np.sqrt((y * y).sum(-1, keepdims=True)), EPS)
    return artanh(np.clip(sqc * n, 0.0, 1.0 - 1e-6)) * y / (sqc * n)


def exp0(v):
    sqc = np.sqrt(C_CURV)
    n = np.maximum(np.sqrt((v * v).sum(-1, keepdims=True)), EPS)
    return np.tanh(sqc * n) * v / (sqc * n)


def setup_inputs():
    s = mx_kscale(C)
    rho = np.sqrt(np.mean(s * s))
    raw = np.random.uniform(0.0, 1.0, (B, C, H, W)) * s[None, :, None, None]
    r = np.random.uniform(0.2, 0.85, (B, 1, H, W))
    x = raw / np.sqrt((raw * raw).sum(1, keepdims=True)) * r / np.sqrt(C_CURV)
    return {"x": bf(x),
            "Wk": bf(np.random.standard_normal((KH * KW, O, C)) * 2.1 / np.sqrt(KH * KW * O) * rho / s),
            "bias": bf(np.random.standard_normal(O) * 5.0 / np.sqrt(O))}


def reference(x, Wk, bias):
    Hout, Wout = H + 2 * PAD - KH + 1, W + 2 * PAD - KW + 1
    u = log0(np.moveaxis(f64(x), 1, -1)).reshape(B * H * W, C)
    w = f64(Wk).transpose(2, 0, 1).reshape(C, KH * KW * O)
    y = mxq(u, 1, "e4m3") @ mxq(w, 0, "e4m3")
    yp = np.pad(y.reshape(B, H, W, KH * KW, O), ((0, 0), (PAD, PAD), (PAD, PAD), (0, 0), (0, 0)))
    v = sum(yp[:, i:i + Hout, j:j + Wout, KW * i + j, :] for i in range(KH) for j in range(KW))
    v = np.maximum(v + f64(bias), 0.0)
    out = exp0(v)
    return np.transpose(out, (0, 3, 1, 2))

@@ -1,0 +1,430 @@
+from contextlib import ExitStack
+
+import concourse.bass as bass
+import concourse.mybir as mybir
+import concourse.tile as tile
+from concourse.masks import make_identity
+
+F32 = mybir.dt.float32
+BF16 = mybir.dt.bfloat16
+U32 = mybir.dt.uint32
+U8 = mybir.dt.uint8
+I32 = mybir.dt.int32
+FP8X4 = mybir.dt.float8_e4m3fn_x4
+ALU = mybir.AluOpType
+ACT = mybir.ActivationFunctionType
+AX = mybir.AxisListType
+
+P = 128
+B, C, O, H, W = 4, 512, 512, 16, 16
+HW = H * W
+ROW = B * W
+NPOS = 9
+FLOPS = 2 * B * HW * C * NPOS * O
+
+
+def tile_pvconv2d_kernel(tc, x, Wk, bias, out):
+    nc = tc.nc
+    with ExitStack() as ctx:
+        const = ctx.enter_context(tc.tile_pool(name="const", bufs=1))
+        big = ctx.enter_context(tc.tile_pool(name="big", bufs=1))
+        stage = ctx.enter_context(tc.tile_pool(name="stage", bufs=3))
+        small = ctx.enter_context(tc.tile_pool(name="small", bufs=1))
+        tsmall = ctx.enter_context(tc.tile_pool(name="tsmall", bufs=4))
+        ps_hd = ctx.enter_context(tc.psum_pool(name="ps_hd", bufs=2))
+        ps_wt = ctx.enter_context(tc.psum_pool(name="ps_wt", bufs=3))
+        ps_acc = ctx.enter_context(tc.psum_pool(name="ps_acc", bufs=3))
+
+        x_sb = big.tile([P, B, 4, HW], BF16)
+        w_sb = [big.tile([P, 4 * C], BF16, name="w_sb%d" % k) for k in range(NPOS)]
+        wq = [big.tile([P, O], U32, name="wq%d" % k, align_bytes=64) for k in range(NPOS)]
+        ws = [big.tile([P, O], U8, name="ws%d" % k, align_bytes=64) for k in range(NPOS)]
+        g_t = [big.tile([P, H, B, W, 4], BF16, name="g%d" % j, align_bytes=64) for j in range(3)]
+        uq = [big.tile([P, (H + 2) * ROW], U32, name="uq%d" % j, align_bytes=64) for j in range(3)]
+        us = [big.tile([P, (H + 2) * ROW], U8, name="us%d" % j, align_bytes=64) for j in range(3)]
+        o_sb = big.tile([P, B, 4, HW], F32)
+        out_v = out.rearrange("b (n ot) h w -> b n ot (h w)", ot=4)
+        ident = const.tile([P, P], F32)
+        perm = const.tile([P, P], F32)
+        half = const.tile([P, 8], F32)
+        mhalf = const.tile([P, 8], F32)
+        ones_bf = const.tile([P, P], BF16)
+        bias_row = const.tile([P, O], BF16)
+        bias_bc = const.tile([P, O], F32)
+        junk = const.tile([P, 8], F32)
+        flat = [g_t[j][:].rearrange("p h b w t -> p (h b) (w t)") for j in range(3)]
+        line = [g_t[j][:].rearrange("p h b w t -> p (h b w t)") for j in range(3)]
+
+        for b in range(B):
+            nc.sync.dma_start(
+                out=x_sb[:, b].rearrange("p t q -> p (t q)"),
+                in_=x[b].rearrange("(p t) h w -> p (t h w)", t=4),
+            )
+        for k in range(NPOS):
+            nc.sync.dma_start(out=w_sb[k][:], in_=Wk[k].rearrange("(n ot) c -> n (ot c)", ot=4))
+        make_identity(nc, ident[:])
+        nc.gpsimd.memset(half[:], 0.5)
+        nc.gpsimd.memset(mhalf[:], -0.5)
+        nc.gpsimd.memset(bias_row[:], 0.0)
+        nc.scalar.dma_start(out=bias_row[0:1, :], in_=bias.unsqueeze(0))
+        nc.gpsimd.memset(ones_bf[:], 1.0)
+        nc.gpsimd.tensor_copy(
+            out=perm[:].rearrange("p (b hh w) -> p b hh w", b=B, hh=2),
+            in_=ident[:].rearrange("p (hh b w) -> p b hh w", hh=2, b=B),
+        )
+        nc.scalar.activation(out=junk[:], in_=half[:], func=ACT.Ln)
+        for j in range(3):
+            nc.vector.memset(us[j][:].bitcast(I32), 0)
+            nc.vector.memset(uq[j][:, 0:ROW].bitcast(I32), 0)
+            nc.vector.memset(uq[j][:, (H + 1) * ROW:(H + 2) * ROW].bitcast(I32), 0)
+        nc.vector.memset(g_t[0][:], 0.0)
+        nc.vector.memset(g_t[2][:], 0.0)
+
+        n2 = [small.tile([P, 4], F32, name="n2_%d" % g) for g in range(2)]
+        n2c = [small.tile([P, 4], F32, name="n2c_%d" % g) for g in range(2)]
+        nrm = [small.tile([P, 4], F32, name="nrm_%d" % g) for g in range(2)]
+        z = [small.tile([P, 4], F32, name="z_%d" % g) for g in range(2)]
+        l1 = [small.tile([P, 4], F32, name="l1_%d" % g) for g in range(2)]
+        l2 = [small.tile([P, 4], F32, name="l2_%d" % g) for g in range(2)]
+        rec = [small.tile([P, 4], F32, name="rec_%d" % g) for g in range(2)]
+        dl = [small.tile([P, 4], F32, name="dl_%d" % g) for g in range(2)]
+        s = [small.tile([P, 4], F32, name="s_%d" % g) for g in range(2)]
+        grams = {}
+        sbc = {}
+
+        def gram_pe(g):
+            grams[g] = ps_hd.tile([P, 4, P], F32, tag="hd", name="gram")
+            for mm in range(4):
+                b, hf = divmod(4 * g + mm, 2)
+                for t in range(4):
+                    blk = x_sb[:, b, t, hf * P:(hf + 1) * P]
+                    nc.tensor.matmul(out=grams[g][:, mm, :], lhsT=blk, rhs=blk, start=(t == 0), stop=(t == 3))
+
+        def gram_diag(g):
+            dg = stage.tile([P, 4, P], F32, tag="dg")
+            nc.vector.tensor_tensor(
+                out=dg[:], in0=grams[g][:], in1=ident[:].unsqueeze(1).to_broadcast([P, 4, P]), op=ALU.mult
+            )
+            nc.vector.tensor_reduce(out=n2[g][:], in_=dg[:], axis=AX.X, op=ALU.add)
+            nc.vector.tensor_scalar(out=n2c[g][:], in0=n2[g][:], scalar1=1e-14, scalar2=None, op0=ALU.max)
+
+        def c_pow(g):
+            nc.gpsimd.tensor_tensor(out=nrm[g][:], in0=n2c[g][:], in1=half[:, 0:4], op=ALU.pow)
+
+        def c_z(g):
+            nc.vector.tensor_scalar(
+                out=z[g][:], in0=nrm[g][:], scalar1=0.1, scalar2=1.0 - 1e-6, op0=ALU.mult, op1=ALU.min
+            )
+            nc.vector.reciprocal(out=rec[g][:], in_=nrm[g][:])
+
+        def c_ln(g):
+            nc.scalar.activation(out=l1[g][:], in_=z[g][:], func=ACT.Ln, bias=1.0, scale=1.0)
+            nc.scalar.activation(out=l2[g][:], in_=z[g][:], func=ACT.Ln, bias=1.0, scale=-1.0)
+
+        def c_s(g):
+            nc.vector.tensor_tensor(out=dl[g][:], in0=l1[g][:], in1=l2[g][:], op=ALU.subtract)
+            nc.vector.scalar_tensor_tensor(
+                out=s[g][:], in0=dl[g][:], scalar=5.0, in1=rec[g][:], op0=ALU.mult, op1=ALU.mult
+            )
+
+        def spread(g):
+            sbc[g] = ps_hd.tile([P, 4 * P], F32, tag="hd", name="sbc")
+            for mm in range(4):
+                nc.tensor.transpose(
+                    sbc[g][:, mm * P:(mm + 1) * P], s[g][:, mm:mm + 1].to_broadcast([P, P]), ident[:]
+                )
+
+        def u_mul(h0, nh, bs):
+            for b in bs:
+                nc.vector.tensor_tensor(
+                    out=g_t[1][:, h0:h0 + nh, b, :, :],
+                    in0=x_sb[:, b, :, h0 * W:(h0 + nh) * W].rearrange("p t (h w) -> p h w t", h=nh),
+                    in1=sbc[b // 2][:, (b % 2) * HW + h0 * W:(b % 2) * HW + (h0 + nh) * W]
+                    .rearrange("p (h w) -> p h w", h=nh)
+                    .unsqueeze(3)
+                    .to_broadcast([P, nh, W, 4]),
+                    op=ALU.mult,
+                )
+
+        def u_shift(h0, nh):
+            r0, r1 = h0 * B, (h0 + nh) * B
+            nc.scalar.copy(out=flat[0][:, r0:r1, 4:64], in_=flat[1][:, r0:r1, 0:60])
+            nc.scalar.copy(out=flat[2][:, r0:r1, 0:60], in_=flat[1][:, r0:r1, 4:64])
+
+        def u_quant(h0, nh, js):
+            for j in js:
+                nc.vector.quantize_mx(
+                    out=uq[j][:, (h0 + 1) * ROW:(h0 + nh + 1) * ROW].bitcast(FP8X4),
+                    scales=us[j][:, (h0 + 1) * ROW:(h0 + nh + 1) * ROW],
+                    in_=line[j][:, h0 * ROW * 4:(h0 + nh) * ROW * 4],
+                )
+
+        def bias_pe():
+            pb = ps_wt.tile([P, O], F32, tag="wt")
+            nc.tensor.matmul(out=pb[:], lhsT=ones_bf[:], rhs=bias_row[:], start=True, stop=True)
+            return pb
+
+        def bias_out(pb):
+            nc.scalar.copy(
+                out=bias_bc[:].rearrange("p (ot n) -> p ot n", ot=4),
+                in_=pb[:].rearrange("p (n ot) -> p ot n", ot=4),
+            )
+
+        wts = {}
+        wgs = {}
+
+        def w_pe(k, hhs=(0, 1)):
+            wf = w_sb[k][:].bitcast(F32)
+            for hh in hhs:
+                wt = ps_wt.tile([P, 2, 2 * P], F32, tag="wt")
+                for u in range(2):
+                    for o2 in range(2):
+                        ot = 2 * hh + o2
+                        nc.tensor.transpose(
+                            wt[:, u, o2 * P:(o2 + 1) * P],
+                            wf[:, 256 * ot + u:256 * (ot + 1):2],
+                            ident[:],
+                        )
+                wts[(k, hh)] = wt
+
+        def w_out(k, hh, eng):
+            if hh == 0:
+                wgs[k] = stage.tile([P, 4 * O], BF16, tag="wg", align_bytes=64, name="wg")
+            dst = wgs[k][:].bitcast(F32)[:, hh * 512:(hh + 1) * 512].rearrange("p (c u) -> p c u", u=2)
+            src = wts[(k, hh)][:].rearrange("p u c -> p c u")
+            if eng == "v":
+                nc.vector.tensor_copy(out=dst, in_=src)
+            else:
+                nc.scalar.copy(out=dst, in_=src)
+
+        def w_quant(k):
+            nc.vector.quantize_mx(out=wq[k][:].bitcast(FP8X4), scales=ws[k][:], in_=wgs[k][:])
+
+        accs = {}
+        done = {}
+
+        def mx(T, ks):
+            if T not in accs:
+                if T in (3, 4):
+                    accs[T] = ps_hd.tile([P, O], F32, tag="hd", name="acc_hd")
+                else:
+                    accs[T] = ps_acc.tile([P, O], F32, tag="acc", name="acc")
+                done[T] = 0
+            for k in ks:
+                done[T] += 1
+                i, j = divmod(k, 3)
+                c0 = (2 * T + i) * ROW
+                nc.tensor.matmul_mx(
+                    out=accs[T][:],
+                    lhsT=uq[j][:, c0:c0 + P].bitcast(FP8X4),
+                    lhsT_scale=us[j][:, c0:c0 + P],
+                    rhs=wq[k][:].bitcast(FP8X4),
+                    rhs_scale=ws[k][:],
+                    start=(done[T] == 1),
+                    stop=(done[T] == NPOS),
+                )
+
+        tl = {}
+
+        def tail_a(T):
+            t_sb = stage.tile([P, O], F32, tag="t")
+            nc.vector.tensor_tensor(out=t_sb[:], in0=accs[T][:], in1=bias_bc[:], op=ALU.add)
+            sq = stage.tile([P, O], F32, tag="sq")
+            m2 = tsmall.tile([P, 1], F32, tag="m2")
+            nc.vector.scalar_tensor_tensor(
+                out=sq[:], in0=t_sb[:], scalar=0.0, in1=t_sb[:], op0=ALU.max, op1=ALU.mult, accum_out=m2[:]
+            )
+            a2 = tsmall.tile([P, 1], F32, tag="a2")
+            nc.vector.tensor_scalar(out=a2[:], in0=m2[:], scalar1=1e-14, scalar2=0.01, op0=ALU.max, op1=ALU.mult)
+            qv = tsmall.tile([P, 1], F32, tag="qv")
+            nc.gpsimd.tensor_tensor(out=qv[:], in0=a2[:], in1=mhalf[:, 0:1], op=ALU.pow)
+            tl[T] = (t_sb, a2, qv)
+
+        def tail_b(T):
+            t_sb, a2, qv = tl[T]
+            th = tsmall.tile([P, 1], F32, tag="th")
+            nc.scalar.activation(out=th[:], in_=a2[:], func=ACT.Tanh, scale=qv[:, 0:1])
+            gs = tsmall.tile([P, 1], F32, tag="gs")
+            nc.scalar.activation(out=gs[:], in_=th[:], func=ACT.Copy, scale=qv[:, 0:1])
+            rs = stage.tile([P, O], F32, tag="rs")
+            nc.scalar.activation(out=rs[:], in_=t_sb[:], func=ACT.Relu, scale=gs[:, 0:1])
+            tl[T] = rs
+
+        def tail_pe(T):
+            rs = tl[T]
+            pt = ps_wt.tile([P, O], F32, tag="wt")
+            for ot in range(4):
+                nc.tensor.transpose(pt[:, ot * P:(ot + 1) * P], rs[:, ot * P:(ot + 1) * P], perm[:])
+            tl[T] = pt
+
+        def tail_c(T, eng="s"):
+            dst = o_sb[:, :, :, 32 * T:32 * T + 32]
+            src = tl[T][:].rearrange("p (ot b q) -> p b ot q", ot=4, b=B)
+            if eng == "v":
+                nc.vector.tensor_copy(out=dst, in_=src)
+            else:
+                nc.scalar.copy(out=dst, in_=src)
+
+        def last_tile(T):
+            t_sb, a2, qv = tl[T]
+            th = tsmall.tile([P, 1], F32, tag="th")
+            nc.scalar.activation(out=th[:], in_=a2[:], func=ACT.Tanh, scale=qv[:, 0:1])
+            gs = tsmall.tile([P, 1], F32, tag="gs")
+            nc.scalar.activation(out=gs[:], in_=th[:], func=ACT.Copy, scale=qv[:, 0:1])
+            rs_a = stage.tile([P, O // 2], F32, tag="rs_a")
+            rs_b = stage.tile([P, O // 2], F32, tag="rs_b")
+            nc.scalar.activation(out=rs_a[:], in_=t_sb[:, 0:256], func=ACT.Relu, scale=gs[:, 0:1])
+            nc.vector.tensor_scalar(
+                out=rs_b[:], in0=t_sb[:, 256:512], scalar1=gs[:, 0:1], scalar2=0.0, op0=ALU.mult, op1=ALU.max
+            )
+            pt_a = ps_wt.tile([P, O // 2], F32, tag="wt")
+            pt_b = ps_wt.tile([P, O // 2], F32, tag="wt")
+            for o2 in range(2):
+                nc.tensor.transpose(pt_a[:, o2 * P:(o2 + 1) * P], rs_a[:, o2 * P:(o2 + 1) * P], perm[:])
+            for o2 in range(2):
+                nc.tensor.transpose(pt_b[:, o2 * P:(o2 + 1) * P], rs_b[:, o2 * P:(o2 + 1) * P], perm[:])
+            nc.scalar.copy(
+                out=o_sb[:, :, 0:2, 32 * T:32 * T + 32],
+                in_=pt_a[:].rearrange("p (ot b q) -> p b ot q", ot=2, b=B),
+            )
+            nc.vector.tensor_copy(
+                out=o_sb[:, :, 2:4, 32 * T:32 * T + 32],
+                in_=pt_b[:].rearrange("p (ot b q) -> p b ot q", ot=2, b=B),
+            )
+
+        def store(q0, q1):
+            for b in range(B):
+                nc.sync.dma_start(out=out_v[b][:, :, q0:q1], in_=o_sb[:, b, :, q0:q1])
+
+        gram_pe(0)
+        gram_pe(1)
+        pb = bias_pe()
+        bias_out(pb)
+        gram_diag(0)
+        c_pow(0)
+        gram_diag(1)
+        c_pow(1)
+        w_pe(0)
+        w_out(0, 0, "s")
+        w_out(0, 1, "v")
+        w_pe(1)
+        c_z(0)
+        c_ln(0)
+        w_quant(0)
+        c_s(0)
+        w_pe(2, (0,))
+        spread(0)
+        w_out(1, 0, "s")
+        c_z(1)
+        c_ln(1)
+        w_out(1, 1, "s")
+        w_pe(2, (1,))
+        c_s(1)
+        spread(1)
+        w_quant(1)
+        w_out(2, 0, "s")
+        w_pe(3, (0,))
+        w_out(2, 1, "s")
+        w_pe(3, (1,))
+        u_mul(0, 2, (0, 1, 2, 3))
+        u_quant(0, 2, (1,))
+        w_out(3, 0, "s")
+        u_shift(0, 2)
+        w_quant(2)
+        w_out(3, 1, "s")
+        u_quant(0, 2, (0, 2))
+        w_pe(4)
+        mx(0, (1, 0, 2))
+        u_mul(2, 2, (0, 1, 2, 3))
+        u_quant(2, 2, (1,))
+        w_out(4, 0, "s")
+        u_shift(2, 2)
+        w_quant(3)
+        w_out(4, 1, "s")
+        u_quant(2, 2, (0, 2))
+        mx(0, (3,))
+        w_pe(5)
+        mx(1, (1, 0, 2, 3))
+        u_mul(4, 4, (0, 1, 2, 3))
+        w_quant(4)
+        u_quant(4, 4, (1,))
+        w_out(5, 0, "s")
+        w_out(5, 1, "s")
+        u_shift(4, 4)
+        mx(0, (4,))
+        mx(1, (4,))
+        w_pe(6)
+        w_quant(5)
+        u_quant(4, 4, (0, 2))
+        w_out(6, 0, "s")
+        w_out(6, 1, "s")
+        mx(0, (5,))
+        mx(1, (5,))
+        mx(2, (1, 4))
+        w_pe(7)
+        mx(2, (0, 2, 3, 5))
+        u_mul(8, 4, (0, 1, 2, 3))
+        w_quant(6)
+        w_out(7, 0, "s")
+        w_out(7, 1, "s")
+        w_pe(8)
+        u_quant(8, 4, (1,))
+        u_shift(8, 4)
+        mx(0, (6,))
+        mx(1, (6,))
+        mx(2, (6,))
+        w_quant(7)
+        w_out(8, 0, "s")
+        w_out(8, 1, "s")
+        u_mul(12, 4, (0, 1, 2, 3))
+        mx(0, (7,))
+        mx(1, (7,))
+        mx(2, (7,))
+        w_quant(8)
+        u_quant(8, 4, (0, 2))
+        u_quant(12, 4, (1,))
+        u_shift(12, 4)
+        mx(0, (8,))
+        mx(1, (8,))
+        mx(2, (8,))
+        tail_a(0)
+        tail_b(0)
+        tail_a(1)
+        tail_b(1)
+        u_quant(12, 4, (0, 2))
+        mx(3, range(9))
+        tail_a(2)
+        tail_b(2)
+        mx(4, range(9))
+        tail_pe(0)
+        tail_pe(1)
+        tail_c(0)
+        tail_c(1)
+        store(0, 64)
+        tail_a(3)
+        tail_b(3)
+        mx(5, range(9))
+        tail_a(4)
+        tail_b(4)
+        mx(6, range(9))
+        tail_pe(2)
+        tail_pe(3)
+        tail_c(2)
+        tail_c(3)
+        store(64, 128)
+        tail_a(5)
+        tail_b(5)
+        mx(7, range(9))
+        tail_a(6)
+        tail_b(6)
+        tail_pe(4)
+        tail_pe(5)
+        tail_a(7)
+        tail_c(4, "s")
+        tail_c(5, "v")
+        store(128, 192)
+        tail_pe(6)
+        tail_c(6, "s")
+        store(192, 224)
+        last_tile(7)
+        store(224, 256)

@@ -20,6 +20,7 @@ B, C, O, H, W = 4, 512, 512, 16, 16
 HW = H * W
 ROW = B * W
 NPOS = 9
+W_ORDER = (1, 4, 7, 0, 3, 6, 2, 5, 8)
 FLOPS = 2 * B * HW * C * NPOS * O
 
 
@@ -31,15 +32,16 @@ def tile_pvconv2d_kernel(tc, x, Wk, bias, out):
         stage = ctx.enter_context(tc.tile_pool(name="stage", bufs=3))
         small = ctx.enter_context(tc.tile_pool(name="small", bufs=1))
         tsmall = ctx.enter_context(tc.tile_pool(name="tsmall", bufs=4))
-        ps_hd = ctx.enter_context(tc.psum_pool(name="ps_hd", bufs=2))
         ps_wt = ctx.enter_context(tc.psum_pool(name="ps_wt", bufs=3))
-        ps_acc = ctx.enter_context(tc.psum_pool(name="ps_acc", bufs=3))
+        ps_acc = ctx.enter_context(tc.psum_pool(name="ps_acc", bufs=5))
+        wg_pool = ctx.enter_context(tc.tile_pool(name="wg_pool", bufs=6))
 
         x_sb = big.tile([P, B, 4, HW], BF16)
         w_sb = [big.tile([P, 4 * C], BF16, name="w_sb%d" % k) for k in range(NPOS)]
         wq = [big.tile([P, O], U32, name="wq%d" % k, align_bytes=64) for k in range(NPOS)]
         ws = [big.tile([P, O], U8, name="ws%d" % k, align_bytes=64) for k in range(NPOS)]
-        g_t = [big.tile([P, H, B, W, 4], BF16, name="g%d" % j, align_bytes=64) for j in range(3)]
+        g_t = big.tile([P, H, B, W, 4], BF16, align_bytes=64)
+        warm = const.tile([P, O], BF16)
         uq = [big.tile([P, (H + 2) * ROW], U32, name="uq%d" % j, align_bytes=64) for j in range(3)]
         us = [big.tile([P, (H + 2) * ROW], U8, name="us%d" % j, align_bytes=64) for j in range(3)]
         o_sb = big.tile([P, B, 4, HW], F32)
@@ -52,21 +54,23 @@ def tile_pvconv2d_kernel(tc, x, Wk, bias, out):
         bias_row = const.tile([P, O], BF16)
         bias_bc = const.tile([P, O], F32)
         junk = const.tile([P, 8], F32)
-        flat = [g_t[j][:].rearrange("p h b w t -> p (h b) (w t)") for j in range(3)]
-        line = [g_t[j][:].rearrange("p h b w t -> p (h b w t)") for j in range(3)]
+        line = g_t[:].rearrange("p h b w t -> p (h b w t)")
+        uq_w = [uq[j][:, ROW:(H + 1) * ROW].bitcast(I32).rearrange("p (r w) -> p r w", w=W) for j in range(3)]
+        us_w = [us[j][:, ROW:(H + 1) * ROW].rearrange("p (r w) -> p r w", w=W) for j in range(3)]
 
+        nc.vector.memset(warm[:], 0.0)
+        nc.vector.memset(bias_row[:], 0.0)
+        nc.scalar.dma_start(out=bias_row[0:1, :], in_=bias.unsqueeze(0))
         for b in range(B):
             nc.sync.dma_start(
                 out=x_sb[:, b].rearrange("p t q -> p (t q)"),
                 in_=x[b].rearrange("(p t) h w -> p (t h w)", t=4),
             )
-        for k in range(NPOS):
+        for k in W_ORDER:
             nc.sync.dma_start(out=w_sb[k][:], in_=Wk[k].rearrange("(n ot) c -> n (ot c)", ot=4))
         make_identity(nc, ident[:])
         nc.gpsimd.memset(half[:], 0.5)
         nc.gpsimd.memset(mhalf[:], -0.5)
-        nc.gpsimd.memset(bias_row[:], 0.0)
-        nc.scalar.dma_start(out=bias_row[0:1, :], in_=bias.unsqueeze(0))
         nc.gpsimd.memset(ones_bf[:], 1.0)
         nc.gpsimd.tensor_copy(
             out=perm[:].rearrange("p (b hh w) -> p b hh w", b=B, hh=2),
@@ -75,69 +79,69 @@ def tile_pvconv2d_kernel(tc, x, Wk, bias, out):
         nc.scalar.activation(out=junk[:], in_=half[:], func=ACT.Ln)
         for j in range(3):
             nc.vector.memset(us[j][:].bitcast(I32), 0)
-            nc.vector.memset(uq[j][:, 0:ROW].bitcast(I32), 0)
-            nc.vector.memset(uq[j][:, (H + 1) * ROW:(H + 2) * ROW].bitcast(I32), 0)
-        nc.vector.memset(g_t[0][:], 0.0)
-        nc.vector.memset(g_t[2][:], 0.0)
+            for c0 in (0, (H + 1) * ROW):
+                nc.vector.memset(uq[j][:, c0:c0 + ROW].bitcast(I32), 0)
+        nc.vector.memset(uq_w[0][:, :, 0:1], 0)
+        nc.vector.memset(uq_w[2][:, :, 15:16], 0)
 
         n2 = [small.tile([P, 4], F32, name="n2_%d" % g) for g in range(2)]
-        n2c = [small.tile([P, 4], F32, name="n2c_%d" % g) for g in range(2)]
         nrm = [small.tile([P, 4], F32, name="nrm_%d" % g) for g in range(2)]
-        z = [small.tile([P, 4], F32, name="z_%d" % g) for g in range(2)]
-        l1 = [small.tile([P, 4], F32, name="l1_%d" % g) for g in range(2)]
-        l2 = [small.tile([P, 4], F32, name="l2_%d" % g) for g in range(2)]
+        z = [small.tile([P, 8], F32, name="z_%d" % g) for g in range(2)]
+        lg = [small.tile([P, 8], F32, name="lg_%d" % g) for g in range(2)]
         rec = [small.tile([P, 4], F32, name="rec_%d" % g) for g in range(2)]
         dl = [small.tile([P, 4], F32, name="dl_%d" % g) for g in range(2)]
         s = [small.tile([P, 4], F32, name="s_%d" % g) for g in range(2)]
+        diag = small.tile([P, 8, P], F32)
         grams = {}
         sbc = {}
 
-        def gram_pe(g):
-            grams[g] = ps_hd.tile([P, 4, P], F32, tag="hd", name="gram")
-            for mm in range(4):
-                b, hf = divmod(4 * g + mm, 2)
+        def gram_pe(b):
+            grams[b] = ps_acc.tile([P, 2, P], F32, tag="acc", name="gram")
+            for hf in range(2):
                 for t in range(4):
                     blk = x_sb[:, b, t, hf * P:(hf + 1) * P]
-                    nc.tensor.matmul(out=grams[g][:, mm, :], lhsT=blk, rhs=blk, start=(t == 0), stop=(t == 3))
+                    nc.tensor.matmul(out=grams[b][:, hf, :], lhsT=blk, rhs=blk, start=(t == 0), stop=(t == 3))
 
-        def gram_diag(g):
-            dg = stage.tile([P, 4, P], F32, tag="dg")
-            nc.vector.tensor_tensor(
-                out=dg[:], in0=grams[g][:], in1=ident[:].unsqueeze(1).to_broadcast([P, 4, P]), op=ALU.mult
-            )
-            nc.vector.tensor_reduce(out=n2[g][:], in_=dg[:], axis=AX.X, op=ALU.add)
-            nc.vector.tensor_scalar(out=n2c[g][:], in0=n2[g][:], scalar1=1e-14, scalar2=None, op0=ALU.max)
+        def gram_diag(b):
+            g, h2 = divmod(b, 2)
+            for hf in range(2):
+                m = 2 * h2 + hf
+                nc.vector.scalar_tensor_tensor(
+                    out=diag[:, 4 * g + m, :], in0=grams[b][:, hf, :], scalar=1e-14, in1=ident[:],
+                    op0=ALU.add, op1=ALU.mult, accum_out=n2[g][:, m:m + 1],
+                )
 
         def c_pow(g):
-            nc.gpsimd.tensor_tensor(out=nrm[g][:], in0=n2c[g][:], in1=half[:, 0:4], op=ALU.pow)
+            nc.gpsimd.tensor_tensor(out=nrm[g][:], in0=n2[g][:], in1=half[:, 0:4], op=ALU.pow)
 
         def c_z(g):
+            lim = 1.0 - 1e-6
             nc.vector.tensor_scalar(
-                out=z[g][:], in0=nrm[g][:], scalar1=0.1, scalar2=1.0 - 1e-6, op0=ALU.mult, op1=ALU.min
+                out=z[g][:, 0:4], in0=nrm[g][:], scalar1=0.1, scalar2=lim, op0=ALU.mult, op1=ALU.min
             )
+            nc.vector.tensor_scalar(
+                out=z[g][:, 4:8], in0=nrm[g][:], scalar1=-0.1, scalar2=-lim, op0=ALU.mult, op1=ALU.max
+            )
+            nc.scalar.activation(out=lg[g][:], in_=z[g][:], func=ACT.Ln, bias=1.0, scale=1.0)
             nc.vector.reciprocal(out=rec[g][:], in_=nrm[g][:])
 
-        def c_ln(g):
-            nc.scalar.activation(out=l1[g][:], in_=z[g][:], func=ACT.Ln, bias=1.0, scale=1.0)
-            nc.scalar.activation(out=l2[g][:], in_=z[g][:], func=ACT.Ln, bias=1.0, scale=-1.0)
-
         def c_s(g):
-            nc.vector.tensor_tensor(out=dl[g][:], in0=l1[g][:], in1=l2[g][:], op=ALU.subtract)
+            nc.vector.tensor_tensor(out=dl[g][:], in0=lg[g][:, 0:4], in1=lg[g][:, 4:8], op=ALU.subtract)
             nc.vector.scalar_tensor_tensor(
                 out=s[g][:], in0=dl[g][:], scalar=5.0, in1=rec[g][:], op0=ALU.mult, op1=ALU.mult
             )
 
         def spread(g):
-            sbc[g] = ps_hd.tile([P, 4 * P], F32, tag="hd", name="sbc")
+            sbc[g] = ps_acc.tile([P, 4 * P], F32, tag="acc", name="sbc")
             for mm in range(4):
                 nc.tensor.transpose(
                     sbc[g][:, mm * P:(mm + 1) * P], s[g][:, mm:mm + 1].to_broadcast([P, P]), ident[:]
                 )
 
-        def u_mul(h0, nh, bs):
-            for b in bs:
+        def u_mul(h0, nh):
+            for b in range(B):
                 nc.vector.tensor_tensor(
-                    out=g_t[1][:, h0:h0 + nh, b, :, :],
+                    out=g_t[:, h0:h0 + nh, b, :, :],
                     in0=x_sb[:, b, :, h0 * W:(h0 + nh) * W].rearrange("p t (h w) -> p h w t", h=nh),
                     in1=sbc[b // 2][:, (b % 2) * HW + h0 * W:(b % 2) * HW + (h0 + nh) * W]
                     .rearrange("p (h w) -> p h w", h=nh)
@@ -146,21 +150,21 @@ def tile_pvconv2d_kernel(tc, x, Wk, bias, out):
                     op=ALU.mult,
                 )
 
-        def u_shift(h0, nh):
-            r0, r1 = h0 * B, (h0 + nh) * B
-            nc.scalar.copy(out=flat[0][:, r0:r1, 4:64], in_=flat[1][:, r0:r1, 0:60])
-            nc.scalar.copy(out=flat[2][:, r0:r1, 0:60], in_=flat[1][:, r0:r1, 4:64])
+        def u_shift(h0, nh, j):
+            r = slice(h0 * B, (h0 + nh) * B)
+            dst, src = (slice(1, 16), slice(0, 15)) if j == 0 else (slice(0, 15), slice(1, 16))
+            nc.vector.tensor_copy(out=uq_w[j][:, r, dst], in_=uq_w[1][:, r, src])
+            nc.vector.tensor_copy(out=us_w[j][:, r, dst], in_=us_w[1][:, r, src])
 
-        def u_quant(h0, nh, js):
-            for j in js:
-                nc.vector.quantize_mx(
-                    out=uq[j][:, (h0 + 1) * ROW:(h0 + nh + 1) * ROW].bitcast(FP8X4),
-                    scales=us[j][:, (h0 + 1) * ROW:(h0 + nh + 1) * ROW],
-                    in_=line[j][:, h0 * ROW * 4:(h0 + nh) * ROW * 4],
-                )
+        def u_quant(h0, nh):
+            nc.vector.quantize_mx(
+                out=uq[1][:, (h0 + 1) * ROW:(h0 + nh + 1) * ROW].bitcast(FP8X4),
+                scales=us[1][:, (h0 + 1) * ROW:(h0 + nh + 1) * ROW],
+                in_=line[:, h0 * ROW * 4:(h0 + nh) * ROW * 4],
+            )
 
         def bias_pe():
-            pb = ps_wt.tile([P, O], F32, tag="wt")
+            pb = ps_acc.tile([P, O], F32, tag="acc")
             nc.tensor.matmul(out=pb[:], lhsT=ones_bf[:], rhs=bias_row[:], start=True, stop=True)
             return pb
 
@@ -189,7 +193,7 @@ def tile_pvconv2d_kernel(tc, x, Wk, bias, out):
 
         def w_out(k, hh, eng):
             if hh == 0:
-                wgs[k] = stage.tile([P, 4 * O], BF16, tag="wg", align_bytes=64, name="wg")
+                wgs[k] = wg_pool.tile([P, 4 * O], BF16, tag="wg", align_bytes=64, name="wg")
             dst = wgs[k][:].bitcast(F32)[:, hh * 512:(hh + 1) * 512].rearrange("p (c u) -> p c u", u=2)
             src = wts[(k, hh)][:].rearrange("p u c -> p c u")
             if eng == "v":
@@ -205,10 +209,7 @@ def tile_pvconv2d_kernel(tc, x, Wk, bias, out):
 
         def mx(T, ks):
             if T not in accs:
-                if T in (3, 4):
-                    accs[T] = ps_hd.tile([P, O], F32, tag="hd", name="acc_hd")
-                else:
-                    accs[T] = ps_acc.tile([P, O], F32, tag="acc", name="acc")
+                accs[T] = ps_acc.tile([P, O], F32, tag="acc", name="acc")
                 done[T] = 0
             for k in ks:
                 done[T] += 1
@@ -296,127 +297,73 @@ def tile_pvconv2d_kernel(tc, x, Wk, bias, out):
             for b in range(B):
                 nc.sync.dma_start(out=out_v[b][:, :, q0:q1], in_=o_sb[:, b, :, q0:q1])
 
-        gram_pe(0)
-        gram_pe(1)
-        pb = bias_pe()
+        for n in range(4):
+            pw = ps_wt.tile([P, O], F32, tag="wt", name="pw")
+            nc.tensor.matmul(out=pw[:], lhsT=warm[:, 0:P], rhs=warm[:], start=True, stop=True)
+        for b in range(4):
+            gram_pe(b)
+            gram_diag(b)
+            if b % 2 == 1:
+                c_pow(b // 2)
+        for n in range(3):
+            k = W_ORDER[n]
+            w_pe(k)
+            w_out(k, 0, "s")
+            w_out(k, 1, "s")
+            if n == 0:
+                c_z(0)
+                c_s(0)
+                spread(0)
+                c_z(1)
+                c_s(1)
+                spread(1)
+        for h0 in range(0, H, 4):
+            u_mul(h0, 4)
+            u_quant(h0, 4)
+            if h0 < 12:
+                w_quant(W_ORDER[h0 // 4])
+        for n in range(3, 9):
+            k = W_ORDER[n]
+            w_pe(k)
+            w_out(k, 0, "s")
+            w_out(k, 1, "s")
+            if n == 3:
+                pb = bias_pe()
         bias_out(pb)
-        gram_diag(0)
-        c_pow(0)
-        gram_diag(1)
-        c_pow(1)
-        w_pe(0)
-        w_out(0, 0, "s")
-        w_out(0, 1, "v")
-        w_pe(1)
-        c_z(0)
-        c_ln(0)
-        w_quant(0)
-        c_s(0)
-        w_pe(2, (0,))
-        spread(0)
-        w_out(1, 0, "s")
-        c_z(1)
-        c_ln(1)
-        w_out(1, 1, "s")
-        w_pe(2, (1,))
-        c_s(1)
-        spread(1)
-        w_quant(1)
-        w_out(2, 0, "s")
-        w_pe(3, (0,))
-        w_out(2, 1, "s")
-        w_pe(3, (1,))
-        u_mul(0, 2, (0, 1, 2, 3))
-        u_quant(0, 2, (1,))
-        w_out(3, 0, "s")
-        u_shift(0, 2)
-        w_quant(2)
-        w_out(3, 1, "s")
-        u_quant(0, 2, (0, 2))
-        w_pe(4)
-        mx(0, (1, 0, 2))
-        u_mul(2, 2, (0, 1, 2, 3))
-        u_quant(2, 2, (1,))
-        w_out(4, 0, "s")
-        u_shift(2, 2)
-        w_quant(3)
-        w_out(4, 1, "s")
-        u_quant(2, 2, (0, 2))
-        mx(0, (3,))
-        w_pe(5)
-        mx(1, (1, 0, 2, 3))
-        u_mul(4, 4, (0, 1, 2, 3))
-        w_quant(4)
-        u_quant(4, 4, (1,))
-        w_out(5, 0, "s")
-        w_out(5, 1, "s")
-        u_shift(4, 4)
-        mx(0, (4,))
-        mx(1, (4,))
-        w_pe(6)
-        w_quant(5)
-        u_quant(4, 4, (0, 2))
-        w_out(6, 0, "s")
-        w_out(6, 1, "s")
-        mx(0, (5,))
-        mx(1, (5,))
-        mx(2, (1, 4))
-        w_pe(7)
-        mx(2, (0, 2, 3, 5))
-        u_mul(8, 4, (0, 1, 2, 3))
-        w_quant(6)
-        w_out(7, 0, "s")
-        w_out(7, 1, "s")
-        w_pe(8)
-        u_quant(8, 4, (1,))
-        u_shift(8, 4)
-        mx(0, (6,))
-        mx(1, (6,))
-        mx(2, (6,))
-        w_quant(7)
-        w_out(8, 0, "s")
-        w_out(8, 1, "s")
-        u_mul(12, 4, (0, 1, 2, 3))
-        mx(0, (7,))
-        mx(1, (7,))
-        mx(2, (7,))
-        w_quant(8)
-        u_quant(8, 4, (0, 2))
-        u_quant(12, 4, (1,))
-        u_shift(12, 4)
-        mx(0, (8,))
-        mx(1, (8,))
-        mx(2, (8,))
-        tail_a(0)
-        tail_b(0)
-        tail_a(1)
-        tail_b(1)
-        u_quant(12, 4, (0, 2))
-        mx(3, range(9))
-        tail_a(2)
-        tail_b(2)
-        mx(4, range(9))
+        for k in (1, 4, 7):
+            for T in range(5):
+                mx(T, (k,))
+        for h0 in range(0, H, 8):
+            u_shift(h0, 8, 0)
+        for k in (0, 3, 6):
+            w_quant(k)
+            for T in range(5):
+                mx(T, (k,))
+        for h0 in range(0, H, 8):
+            u_shift(h0, 8, 2)
+        for k in (2, 5, 8):
+            w_quant(k)
+        for T in range(5):
+            mx(T, (2, 5, 8))
+            tail_a(T)
+            tail_b(T)
+        mx(5, range(9))
         tail_pe(0)
         tail_pe(1)
         tail_c(0)
         tail_c(1)
         store(0, 64)
-        tail_a(3)
-        tail_b(3)
-        mx(5, range(9))
-        tail_a(4)
-        tail_b(4)
+        tail_a(5)
+        tail_b(5)
         mx(6, range(9))
         tail_pe(2)
         tail_pe(3)
         tail_c(2)
         tail_c(3)
         store(64, 128)
-        tail_a(5)
-        tail_b(5)
-        mx(7, range(9))
         tail_a(6)
         tail_b(6)
+        mx(7, range(9))
         tail_pe(4)
         tail_pe(5)
         tail_a(7)

@@ -31,10 +31,12 @@ def tile_pvconv2d_kernel(tc, x, Wk, bias, out):
         big = ctx.enter_context(tc.tile_pool(name="big", bufs=1))
         stage = ctx.enter_context(tc.tile_pool(name="stage", bufs=3))
         small = ctx.enter_context(tc.tile_pool(name="small", bufs=1))
-        tsmall = ctx.enter_context(tc.tile_pool(name="tsmall", bufs=4))
+        t_pool = ctx.enter_context(tc.tile_pool(name="t_pool", bufs=5))
+        rs_pool = ctx.enter_context(tc.tile_pool(name="rs_pool", bufs=6))
+        tsmall = ctx.enter_context(tc.tile_pool(name="tsmall", bufs=8))
         ps_wt = ctx.enter_context(tc.psum_pool(name="ps_wt", bufs=3))
         ps_acc = ctx.enter_context(tc.psum_pool(name="ps_acc", bufs=5))
-        wg_pool = ctx.enter_context(tc.tile_pool(name="wg_pool", bufs=6))
+        wg_pool = ctx.enter_context(tc.tile_pool(name="wg_pool", bufs=9))
 
         x_sb = big.tile([P, B, 4, HW], BF16)
         w_sb = [big.tile([P, 4 * C], BF16, name="w_sb%d" % k) for k in range(NPOS)]
@@ -61,13 +63,20 @@ def tile_pvconv2d_kernel(tc, x, Wk, bias, out):
         nc.vector.memset(warm[:], 0.0)
         nc.vector.memset(bias_row[:], 0.0)
         nc.scalar.dma_start(out=bias_row[0:1, :], in_=bias.unsqueeze(0))
-        for b in range(B):
+        def load_x(b):
             nc.sync.dma_start(
                 out=x_sb[:, b].rearrange("p t q -> p (t q)"),
                 in_=x[b].rearrange("(p t) h w -> p (t h w)", t=4),
             )
-        for k in W_ORDER:
+
+        def load_w(k):
             nc.sync.dma_start(out=w_sb[k][:], in_=Wk[k].rearrange("(n ot) c -> n (ot c)", ot=4))
+
+        for b in range(B):
+            load_x(b)
+        load_w(W_ORDER[0])
+        for k in W_ORDER[1:]:
+            load_w(k)
         make_identity(nc, ident[:])
         nc.gpsimd.memset(half[:], 0.5)
         nc.gpsimd.memset(mhalf[:], -0.5)
@@ -86,7 +95,7 @@ def tile_pvconv2d_kernel(tc, x, Wk, bias, out):
 
         n2 = [small.tile([P, 4], F32, name="n2_%d" % g) for g in range(2)]
         nrm = [small.tile([P, 4], F32, name="nrm_%d" % g) for g in range(2)]
-        z = [small.tile([P, 8], F32, name="z_%d" % g) for g in range(2)]
+        z = [small.tile([P, 4], F32, name="z_%d" % g) for g in range(2)]
         lg = [small.tile([P, 8], F32, name="lg_%d" % g) for g in range(2)]
         rec = [small.tile([P, 4], F32, name="rec_%d" % g) for g in range(2)]
         dl = [small.tile([P, 4], F32, name="dl_%d" % g) for g in range(2)]
@@ -115,14 +124,11 @@ def tile_pvconv2d_kernel(tc, x, Wk, bias, out):
             nc.gpsimd.tensor_tensor(out=nrm[g][:], in0=n2[g][:], in1=half[:, 0:4], op=ALU.pow)
 
         def c_z(g):
-            lim = 1.0 - 1e-6
             nc.vector.tensor_scalar(
-                out=z[g][:, 0:4], in0=nrm[g][:], scalar1=0.1, scalar2=lim, op0=ALU.mult, op1=ALU.min
+                out=z[g][:], in0=nrm[g][:], scalar1=10.0 * (1.0 - 1e-6), scalar2=None, op0=ALU.min
             )
-            nc.vector.tensor_scalar(
-                out=z[g][:, 4:8], in0=nrm[g][:], scalar1=-0.1, scalar2=-lim, op0=ALU.mult, op1=ALU.max
-            )
-            nc.scalar.activation(out=lg[g][:], in_=z[g][:], func=ACT.Ln, bias=1.0, scale=1.0)
+            nc.scalar.activation(out=lg[g][:, 0:4], in_=z[g][:], func=ACT.Ln, bias=1.0, scale=0.1)
+            nc.scalar.activation(out=lg[g][:, 4:8], in_=z[g][:], func=ACT.Ln, bias=1.0, scale=-0.1)
             nc.vector.reciprocal(out=rec[g][:], in_=nrm[g][:])
 
         def c_s(g):
@@ -138,8 +144,8 @@ def tile_pvconv2d_kernel(tc, x, Wk, bias, out):
                     sbc[g][:, mm * P:(mm + 1) * P], s[g][:, mm:mm + 1].to_broadcast([P, P]), ident[:]
                 )
 
-        def u_mul(h0, nh):
-            for b in range(B):
+        def u_mul(h0, nh, bs=(0, 1, 2, 3)):
+            for b in bs:
                 nc.vector.tensor_tensor(
                     out=g_t[:, h0:h0 + nh, b, :, :],
                     in0=x_sb[:, b, :, h0 * W:(h0 + nh) * W].rearrange("p t (h w) -> p h w t", h=nh),
@@ -164,7 +170,7 @@ def tile_pvconv2d_kernel(tc, x, Wk, bias, out):
             )
 
         def bias_pe():
-            pb = ps_acc.tile([P, O], F32, tag="acc")
+            pb = ps_wt.tile([P, O], F32, tag="wt")
             nc.tensor.matmul(out=pb[:], lhsT=ones_bf[:], rhs=bias_row[:], start=True, stop=True)
             return pb
 
@@ -207,47 +213,57 @@ def tile_pvconv2d_kernel(tc, x, Wk, bias, out):
         accs = {}
         done = {}
 
-        def mx(T, ks):
-            if T not in accs:
-                accs[T] = ps_acc.tile([P, O], F32, tag="acc", name="acc")
-                done[T] = 0
+        def mx(T, ks, half=None):
+            key = T if half is None else (T, half)
+            cols = slice(0, O) if half is None else slice(half * 256, half * 256 + 256)
+            if key not in accs:
+                accs[key] = ps_acc.tile([P, O if half is None else 256], F32, tag="acc", name="acc")
+                done[key] = 0
             for k in ks:
-                done[T] += 1
+                done[key] += 1
                 i, j = divmod(k, 3)
                 c0 = (2 * T + i) * ROW
                 nc.tensor.matmul_mx(
-                    out=accs[T][:],
+                    out=accs[key][:],
                     lhsT=uq[j][:, c0:c0 + P].bitcast(FP8X4),
                     lhsT_scale=us[j][:, c0:c0 + P],
-                    rhs=wq[k][:].bitcast(FP8X4),
-                    rhs_scale=ws[k][:],
-                    start=(done[T] == 1),
-                    stop=(done[T] == NPOS),
+                    rhs=wq[k][:, cols].bitcast(FP8X4),
+                    rhs_scale=ws[k][:, cols],
+                    start=(done[key] == 1),
+                    stop=(done[key] == NPOS),
                 )
 
         tl = {}
 
-        def tail_a(T):
-            t_sb = stage.tile([P, O], F32, tag="t")
+        def tail_add(T):
+            t_sb = t_pool.tile([P, O], F32, tag="t")
             nc.vector.tensor_tensor(out=t_sb[:], in0=accs[T][:], in1=bias_bc[:], op=ALU.add)
+            tl[T] = t_sb
+
+        def tail_sq(T):
+            t_sb = tl[T]
             sq = stage.tile([P, O], F32, tag="sq")
             m2 = tsmall.tile([P, 1], F32, tag="m2")
             nc.vector.scalar_tensor_tensor(
                 out=sq[:], in0=t_sb[:], scalar=0.0, in1=t_sb[:], op0=ALU.max, op1=ALU.mult, accum_out=m2[:]
             )
             a2 = tsmall.tile([P, 1], F32, tag="a2")
-            nc.vector.tensor_scalar(out=a2[:], in0=m2[:], scalar1=1e-14, scalar2=0.01, op0=ALU.max, op1=ALU.mult)
+            nc.gpsimd.tensor_scalar(out=a2[:], in0=m2[:], scalar1=1e-14, scalar2=0.01, op0=ALU.max, op1=ALU.mult)
             qv = tsmall.tile([P, 1], F32, tag="qv")
             nc.gpsimd.tensor_tensor(out=qv[:], in0=a2[:], in1=mhalf[:, 0:1], op=ALU.pow)
             tl[T] = (t_sb, a2, qv)
 
-        def tail_b(T):
+        def tail_th(T):
             t_sb, a2, qv = tl[T]
             th = tsmall.tile([P, 1], F32, tag="th")
             nc.scalar.activation(out=th[:], in_=a2[:], func=ACT.Tanh, scale=qv[:, 0:1])
             gs = tsmall.tile([P, 1], F32, tag="gs")
-            nc.scalar.activation(out=gs[:], in_=th[:], func=ACT.Copy, scale=qv[:, 0:1])
-            rs = stage.tile([P, O], F32, tag="rs")
+            nc.gpsimd.tensor_tensor(out=gs[:], in0=th[:], in1=qv[:], op=ALU.mult)
+            tl[T] = (t_sb, gs)
+
+        def tail_relu(T):
+            t_sb, gs = tl[T]
+            rs = rs_pool.tile([P, O], F32, tag="rs")
             nc.scalar.activation(out=rs[:], in_=t_sb[:], func=ACT.Relu, scale=gs[:, 0:1])
             tl[T] = rs
 
@@ -266,38 +282,70 @@ def tile_pvconv2d_kernel(tc, x, Wk, bias, out):
             else:
                 nc.scalar.copy(out=dst, in_=src)
 
-        def last_tile(T):
-            t_sb, a2, qv = tl[T]
+        lh = {}
+
+        def last_a(T, half):
+            cols = slice(half * 256, half * 256 + 256)
+            t_h = stage.tile([P, 256], F32, tag="t_h")
+            nc.vector.tensor_tensor(out=t_h[:], in0=accs[(T, half)][:], in1=bias_bc[:, cols], op=ALU.add)
+            sq_h = stage.tile([P, 256], F32, tag="sq_h")
+            m2_h = tsmall.tile([P, 1], F32, tag="m2_h")
+            nc.vector.scalar_tensor_tensor(
+                out=sq_h[:], in0=t_h[:], scalar=0.0, in1=t_h[:], op0=ALU.max, op1=ALU.mult, accum_out=m2_h[:]
+            )
+            lh[half] = (t_h, m2_h)
+
+        def last_b(T):
+            (t_a, m2_a), (t_b, m2_b) = lh[0], lh[1]
+            a2 = tsmall.tile([P, 1], F32, tag="a2")
+            nc.vector.tensor_scalar(
+                out=a2[:], in0=m2_b[:], scalar1=lh[2][:, 0:1], scalar2=0.01, op0=ALU.add, op1=ALU.mult
+            )
+            qv = tsmall.tile([P, 1], F32, tag="qv")
+            nc.gpsimd.tensor_tensor(out=qv[:], in0=a2[:], in1=mhalf[:, 0:1], op=ALU.pow)
             th = tsmall.tile([P, 1], F32, tag="th")
             nc.scalar.activation(out=th[:], in_=a2[:], func=ACT.Tanh, scale=qv[:, 0:1])
             gs = tsmall.tile([P, 1], F32, tag="gs")
-            nc.scalar.activation(out=gs[:], in_=th[:], func=ACT.Copy, scale=qv[:, 0:1])
-            rs_a = stage.tile([P, O // 2], F32, tag="rs_a")
-            rs_b = stage.tile([P, O // 2], F32, tag="rs_b")
-            nc.scalar.activation(out=rs_a[:], in_=t_sb[:, 0:256], func=ACT.Relu, scale=gs[:, 0:1])
+            nc.gpsimd.tensor_tensor(out=gs[:], in0=th[:], in1=qv[:], op=ALU.mult)
+            lh[3] = gs
+
+        def last_c(T):
+            (t_a, m2_a), (t_b, m2_b), gs = lh[0], lh[1], lh[3]
+            rs_a = stage.tile([P, 256], F32, tag="rs_a")
+            rs_b = stage.tile([P, 256], F32, tag="rs_b")
+            nc.scalar.activation(out=rs_a[:], in_=t_a[:], func=ACT.Relu, scale=gs[:, 0:1])
             nc.vector.tensor_scalar(
-                out=rs_b[:], in0=t_sb[:, 256:512], scalar1=gs[:, 0:1], scalar2=0.0, op0=ALU.mult, op1=ALU.max
+                out=rs_b[:], in0=t_b[:], scalar1=gs[:, 0:1], scalar2=0.0, op0=ALU.mult, op1=ALU.max
             )
-            pt_a = ps_wt.tile([P, O // 2], F32, tag="wt")
-            pt_b = ps_wt.tile([P, O // 2], F32, tag="wt")
-            for o2 in range(2):
-                nc.tensor.transpose(pt_a[:, o2 * P:(o2 + 1) * P], rs_a[:, o2 * P:(o2 + 1) * P], perm[:])
-            for o2 in range(2):
-                nc.tensor.transpose(pt_b[:, o2 * P:(o2 + 1) * P], rs_b[:, o2 * P:(o2 + 1) * P], perm[:])
-            nc.scalar.copy(
-                out=o_sb[:, :, 0:2, 32 * T:32 * T + 32],
-                in_=pt_a[:].rearrange("p (ot b q) -> p b ot q", ot=2, b=B),
-            )
+            pt_a = ps_wt.tile([P, 256], F32, tag="wt")
+            pt_b = ps_wt.tile([P, 256], F32, tag="wt")
+            for pt, rs_h in ((pt_b, rs_b), (pt_a, rs_a)):
+                for o2 in range(2):
+                    nc.tensor.transpose(pt[:, o2 * P:(o2 + 1) * P], rs_h[:, o2 * P:(o2 + 1) * P], perm[:])
             nc.vector.tensor_copy(
                 out=o_sb[:, :, 2:4, 32 * T:32 * T + 32],
                 in_=pt_b[:].rearrange("p (ot b q) -> p b ot q", ot=2, b=B),
             )
+            nc.scalar.copy(
+                out=o_sb[:, :, 0:2, 32 * T:32 * T + 32],
+                in_=pt_a[:].rearrange("p (ot b q) -> p b ot q", ot=2, b=B),
+            )
+
+        def last_floor():
+            m2_f = tsmall.tile([P, 1], F32, tag="m2_f")
+            nc.vector.tensor_scalar(out=m2_f[:], in0=lh[0][1][:], scalar1=1e-14, scalar2=None, op0=ALU.max)
+            lh[2] = m2_f
+
+        def tanh_table(k):
+            nc.scalar.activation(out=junk[:, 0:1], in_=wgs[k][:, 0:1], func=ACT.Tanh)
 
         def store(q0, q1):
             for b in range(B):
                 nc.sync.dma_start(out=out_v[b][:, :, q0:q1], in_=o_sb[:, b, :, q0:q1])
 
-        for n in range(4):
+        ctx.enter_context(tc.manual_schedule())
+        WO = W_ORDER
+        for n in range(3):
             pw = ps_wt.tile([P, O], F32, tag="wt", name="pw")
             nc.tensor.matmul(out=pw[:], lhsT=warm[:, 0:P], rhs=warm[:], start=True, stop=True)
         for b in range(4):
@@ -305,73 +353,142 @@ def tile_pvconv2d_kernel(tc, x, Wk, bias, out):
             gram_diag(b)
             if b % 2 == 1:
                 c_pow(b // 2)
-        for n in range(3):
-            k = W_ORDER[n]
-            w_pe(k)
-            w_out(k, 0, "s")
-            w_out(k, 1, "s")
-            if n == 0:
-                c_z(0)
-                c_s(0)
-                spread(0)
-                c_z(1)
-                c_s(1)
-                spread(1)
-        for h0 in range(0, H, 4):
-            u_mul(h0, 4)
-            u_quant(h0, 4)
-            if h0 < 12:
-                w_quant(W_ORDER[h0 // 4])
-        for n in range(3, 9):
-            k = W_ORDER[n]
-            w_pe(k)
-            w_out(k, 0, "s")
-            w_out(k, 1, "s")
-            if n == 3:
-                pb = bias_pe()
+        w_pe(WO[0])
+        c_z(0)
+        w_out(WO[0], 0, "s")
+        c_s(0)
+        w_out(WO[0], 1, "s")
+        spread(0)
+        c_z(1)
+        w_pe(WO[1])
+        w_out(WO[1], 0, "s")
+        u_mul(0, 4, (0,))
+        c_s(1)
+        spread(1)
+        w_quant(WO[0])
+        u_mul(0, 4, (1, 2, 3))
+        u_quant(0, 4)
+        w_out(WO[1], 1, "s")
+        w_pe(WO[2])
+        w_out(WO[2], 0, "s")
+        w_out(WO[2], 1, "s")
+        w_pe(WO[3])
+        w_out(WO[3], 0, "s")
+        w_out(WO[3], 1, "s")
+        mx(0, WO[0:1])
+        w_pe(WO[4])
+        w_out(WO[4], 0, "s")
+        w_out(WO[4], 1, "s")
+        w_quant(WO[1])
+        u_mul(4, 4)
+        u_quant(4, 4)
+        u_shift(0, 8, 0)
+        mx(0, WO[1:2])
+        w_pe(WO[5], (0,))
+        w_out(WO[5], 0, "s")
+        mx(1, WO[0:1])
+        w_pe(WO[5], (1,))
+        w_out(WO[5], 1, "s")
+        mx(1, WO[1:2])
+        w_quant(WO[2])
+        w_pe(WO[6], (0,))
+        w_out(WO[6], 0, "s")
+        mx(2, WO[0:1])
+        w_pe(WO[6], (1,))
+        w_out(WO[6], 1, "s")
+        mx(2, WO[1:2])
+        w_quant(WO[3])
+        w_quant(WO[4])
+        w_pe(WO[7], (0,))
+        w_out(WO[7], 0, "s")
+        mx(0, WO[2:3])
+        w_pe(WO[7], (1,))
+        w_out(WO[7], 1, "s")
+        mx(1, WO[2:3])
+        u_mul(8, 8)
+        u_quant(8, 8)
+        w_pe(WO[8], (0,))
+        w_out(WO[8], 0, "s")
+        mx(2, WO[2:3])
+        w_pe(WO[8], (1,))
+        w_out(WO[8], 1, "s")
+        pb = bias_pe()
+        tanh_table(WO[8])
         bias_out(pb)
-        for k in (1, 4, 7):
-            for T in range(5):
-                mx(T, (k,))
-        for h0 in range(0, H, 8):
-            u_shift(h0, 8, 0)
-        for k in (0, 3, 6):
-            w_quant(k)
-            for T in range(5):
-                mx(T, (k,))
-        for h0 in range(0, H, 8):
-            u_shift(h0, 8, 2)
-        for k in (2, 5, 8):
-            w_quant(k)
-        for T in range(5):
-            mx(T, (2, 5, 8))
-            tail_a(T)
-            tail_b(T)
-        mx(5, range(9))
+        for n in (3, 4):
+            for T in range(3):
+                mx(T, WO[n:n + 1])
+        for T in (3, 4):
+            mx(T, WO[0:3])
+        w_quant(WO[5])
+        u_shift(8, 8, 0)
+        for T in range(3):
+            mx(T, WO[5:6])
+        u_shift(0, 8, 2)
+        for n in (6, 7, 8):
+            w_quant(WO[n])
+        for T in (3, 4):
+            mx(T, WO[3:6])
+        for T in range(3):
+            mx(T, WO[6:9])
+        u_shift(8, 8, 2)
+        for T in (3, 4):
+            mx(T, WO[6:9])
+        tail_add(0)
+        tail_add(1)
+        tail_sq(0)
+        tail_add(2)
+        tail_sq(1)
+        tail_th(0)
+        tail_add(3)
+        tail_sq(2)
+        tail_th(1)
+        tail_relu(0)
+        mx(5, WO)
+        tail_add(4)
+        tail_sq(3)
+        tail_th(2)
+        tail_relu(1)
+        mx(6, WO[0:3])
         tail_pe(0)
         tail_pe(1)
+        tail_add(5)
+        tail_sq(4)
+        tail_th(3)
+        tail_relu(2)
         tail_c(0)
+        mx(6, WO[3:9])
+        tail_pe(2)
+        tail_sq(5)
+        tail_th(4)
+        tail_relu(3)
         tail_c(1)
         store(0, 64)
-        tail_a(5)
-        tail_b(5)
-        mx(6, range(9))
-        tail_pe(2)
+        mx(7, WO, 0)
         tail_pe(3)
+        tail_add(6)
+        tail_th(5)
+        tail_relu(4)
         tail_c(2)
+        tail_sq(6)
+        mx(7, WO[0:4], 1)
+        tail_pe(4)
+        mx(7, WO[4:9], 1)
+        last_a(7, 0)
+        last_floor()
+        tail_relu(5)
         tail_c(3)
         store(64, 128)
-        tail_a(6)
-        tail_b(6)
-        mx(7, range(9))
-        tail_pe(4)
         tail_pe(5)
-        tail_a(7)
-        tail_c(4, "s")
-        tail_c(5, "v")
+        tail_th(6)
+        tail_c(4)
+        tail_relu(6)
+        last_a(7, 1)
+        tail_c(5)
         store(128, 192)
         tail_pe(6)
-        tail_c(6, "s")
+        last_b(7)
+        tail_c(6, "v")
         store(192, 224)
-        last_tile(7)
+        last_c(7)
         store(224, 256)

@@ -36,6 +36,7 @@ def tile_pvconv2d_kernel(tc, x, Wk, bias, out):
         tsmall = ctx.enter_context(tc.tile_pool(name="tsmall", bufs=8))
         ps_wt = ctx.enter_context(tc.psum_pool(name="ps_wt", bufs=3))
         ps_acc = ctx.enter_context(tc.psum_pool(name="ps_acc", bufs=5))
+        wp_pool = ctx.enter_context(tc.tile_pool(name="wp_pool", bufs=3))
         wg_pool = ctx.enter_context(tc.tile_pool(name="wg_pool", bufs=9))
 
         x_sb = big.tile([P, B, 4, HW], BF16)
@@ -183,6 +184,19 @@ def tile_pvconv2d_kernel(tc, x, Wk, bias, out):
         wts = {}
         wgs = {}
 
+        def warm_pe(n):
+            for m in range(n):
+                pw = ps_wt.tile([P, O], F32, tag="wt", name="pw")
+                nc.tensor.matmul(out=pw[:], lhsT=warm[:, 0:P], rhs=warm[:], start=True, stop=True)
+
+        wps = {}
+
+        def w_perm(k):
+            wps[k] = wp_pool.tile([P, 4, 2, P], F32, tag="wp", name="wp")
+            nc.vector.tensor_copy(
+                out=wps[k][:], in_=w_sb[k][:].bitcast(F32).rearrange("p (ot n u) -> p ot u n", ot=4, u=2)
+            )
+
         def w_pe(k, hhs=(0, 1)):
             wf = w_sb[k][:].bitcast(F32)
             for hh in hhs:
@@ -192,7 +206,7 @@ def tile_pvconv2d_kernel(tc, x, Wk, bias, out):
                         ot = 2 * hh + o2
                         nc.tensor.transpose(
                             wt[:, u, o2 * P:(o2 + 1) * P],
-                            wf[:, 256 * ot + u:256 * (ot + 1):2],
+                            wps[k][:, ot, u, :] if k in wps else wf[:, 256 * ot + u:256 * (ot + 1):2],
                             ident[:],
                         )
                 wts[(k, hh)] = wt
@@ -345,79 +359,82 @@ def tile_pvconv2d_kernel(tc, x, Wk, bias, out):
 
         ctx.enter_context(tc.manual_schedule())
         WO = W_ORDER
-        for n in range(3):
-            pw = ps_wt.tile([P, O], F32, tag="wt", name="pw")
-            nc.tensor.matmul(out=pw[:], lhsT=warm[:, 0:P], rhs=warm[:], start=True, stop=True)
+        warm_pe(3)
         for b in range(4):
             gram_pe(b)
             gram_diag(b)
             if b % 2 == 1:
                 c_pow(b // 2)
+        w_perm(WO[0])
+        warm_pe(2)
         w_pe(WO[0])
         c_z(0)
-        w_out(WO[0], 0, "s")
+        w_perm(WO[1])
         c_s(0)
-        w_out(WO[0], 1, "s")
+        w_out(WO[0], 0, "s")
+        warm_pe(1)
         spread(0)
         c_z(1)
+        w_out(WO[0], 1, "s")
         w_pe(WO[1])
+        warm_pe(1)
         w_out(WO[1], 0, "s")
+        w_perm(WO[2])
         u_mul(0, 4, (0,))
         c_s(1)
         spread(1)
-        w_quant(WO[0])
-        u_mul(0, 4, (1, 2, 3))
-        u_quant(0, 4)
         w_out(WO[1], 1, "s")
         w_pe(WO[2])
+        warm_pe(1)
+        u_mul(0, 4, (1, 2, 3))
+        w_quant(WO[0])
+        u_quant(0, 4)
         w_out(WO[2], 0, "s")
         w_out(WO[2], 1, "s")
-        w_pe(WO[3])
+        w_pe(WO[3], (0,))
+        warm_pe(1)
+        w_pe(WO[3], (1,))
+        warm_pe(1)
         w_out(WO[3], 0, "s")
         w_out(WO[3], 1, "s")
+        w_quant(WO[1])
         mx(0, WO[0:1])
-        w_pe(WO[4])
+        w_pe(WO[4], (0,))
+        warm_pe(1)
+        w_pe(WO[4], (1,))
         w_out(WO[4], 0, "s")
         w_out(WO[4], 1, "s")
-        w_quant(WO[1])
-        u_mul(4, 4)
-        u_quant(4, 4)
-        u_shift(0, 8, 0)
         mx(0, WO[1:2])
-        w_pe(WO[5], (0,))
-        w_out(WO[5], 0, "s")
-        mx(1, WO[0:1])
-        w_pe(WO[5], (1,))
-        w_out(WO[5], 1, "s")
-        mx(1, WO[1:2])
+        u_mul(4, 4)
         w_quant(WO[2])
-        w_pe(WO[6], (0,))
-        w_out(WO[6], 0, "s")
-        mx(2, WO[0:1])
-        w_pe(WO[6], (1,))
-        w_out(WO[6], 1, "s")
-        mx(2, WO[1:2])
+        u_quant(4, 4)
+        w_pe(WO[5])
+        w_out(WO[5], 0, "s")
+        w_out(WO[5], 1, "s")
+        mx(0, WO[2:3])
+        mx(1, WO[0:3])
+        mx(2, WO[0:3])
+        u_shift(0, 8, 0)
         w_quant(WO[3])
         w_quant(WO[4])
-        w_pe(WO[7], (0,))
-        w_out(WO[7], 0, "s")
-        mx(0, WO[2:3])
-        w_pe(WO[7], (1,))
-        w_out(WO[7], 1, "s")
-        mx(1, WO[2:3])
+        w_pe(WO[6])
+        w_out(WO[6], 0, "s")
+        w_out(WO[6], 1, "s")
+        for T in range(3):
+            mx(T, WO[3:4])
         u_mul(8, 8)
         u_quant(8, 8)
-        w_pe(WO[8], (0,))
+        w_pe(WO[7])
+        w_out(WO[7], 0, "s")
+        w_out(WO[7], 1, "s")
+        for T in range(3):
+            mx(T, WO[4:5])
+        w_pe(WO[8])
         w_out(WO[8], 0, "s")
-        mx(2, WO[2:3])
-        w_pe(WO[8], (1,))
         w_out(WO[8], 1, "s")
         pb = bias_pe()
         tanh_table(WO[8])
         bias_out(pb)
-        for n in (3, 4):
-            for T in range(3):
-                mx(T, WO[n:n + 1])
         for T in (3, 4):
             mx(T, WO[0:3])
         w_quant(WO[5])

@@ -1,8 +1,6 @@
 from contextlib import ExitStack
 
-import concourse.bass as bass
 import concourse.mybir as mybir
-import concourse.tile as tile
 from concourse.masks import make_identity
 
 F32 = mybir.dt.float32
@@ -13,14 +11,13 @@ I32 = mybir.dt.int32
 FP8X4 = mybir.dt.float8_e4m3fn_x4
 ALU = mybir.AluOpType
 ACT = mybir.ActivationFunctionType
-AX = mybir.AxisListType
 
 P = 128
 B, C, O, H, W = 4, 512, 512, 16, 16
 HW = H * W
-ROW = B * W
+IMG = (H + 2) * W
 NPOS = 9
-W_ORDER = (1, 4, 7, 0, 3, 6, 2, 5, 8)
+W_ORDER = (4, 1, 7, 3, 0, 6, 5, 2, 8)
 FLOPS = 2 * B * HW * C * NPOS * O
 
 
@@ -34,76 +31,71 @@ def tile_pvconv2d_kernel(tc, x, Wk, bias, out):
         t_pool = ctx.enter_context(tc.tile_pool(name="t_pool", bufs=5))
         rs_pool = ctx.enter_context(tc.tile_pool(name="rs_pool", bufs=6))
         tsmall = ctx.enter_context(tc.tile_pool(name="tsmall", bufs=8))
+        wp_pool = ctx.enter_context(tc.tile_pool(name="wp_pool", bufs=4))
+        wg_pool = ctx.enter_context(tc.tile_pool(name="wg_pool", bufs=9))
         ps_wt = ctx.enter_context(tc.psum_pool(name="ps_wt", bufs=3))
         ps_acc = ctx.enter_context(tc.psum_pool(name="ps_acc", bufs=5))
-        wp_pool = ctx.enter_context(tc.tile_pool(name="wp_pool", bufs=3))
-        wg_pool = ctx.enter_context(tc.tile_pool(name="wg_pool", bufs=9))
 
         x_sb = big.tile([P, B, 4, HW], BF16)
         w_sb = [big.tile([P, 4 * C], BF16, name="w_sb%d" % k) for k in range(NPOS)]
         wq = [big.tile([P, O], U32, name="wq%d" % k, align_bytes=64) for k in range(NPOS)]
         ws = [big.tile([P, O], U8, name="ws%d" % k, align_bytes=64) for k in range(NPOS)]
-        g_t = big.tile([P, H, B, W, 4], BF16, align_bytes=64)
-        warm = const.tile([P, O], BF16)
-        uq = [big.tile([P, (H + 2) * ROW], U32, name="uq%d" % j, align_bytes=64) for j in range(3)]
-        us = [big.tile([P, (H + 2) * ROW], U8, name="us%d" % j, align_bytes=64) for j in range(3)]
+        g_t = big.tile([P, B, HW * 4], BF16, align_bytes=64)
+        uq = big.tile([P, 3, B, IMG], U32, align_bytes=64)
+        us = big.tile([P, 3, 3, B, HW], U8, align_bytes=64)
         o_sb = big.tile([P, B, 4, HW], F32)
         out_v = out.rearrange("b (n ot) h w -> b n ot (h w)", ot=4)
         ident = const.tile([P, P], F32)
-        perm = const.tile([P, P], F32)
         half = const.tile([P, 8], F32)
         mhalf = const.tile([P, 8], F32)
         ones_bf = const.tile([P, P], BF16)
         bias_row = const.tile([P, O], BF16)
         bias_bc = const.tile([P, O], F32)
         junk = const.tile([P, 8], F32)
-        line = g_t[:].rearrange("p h b w t -> p (h b w t)")
-        uq_w = [uq[j][:, ROW:(H + 1) * ROW].bitcast(I32).rearrange("p (r w) -> p r w", w=W) for j in range(3)]
-        us_w = [us[j][:, ROW:(H + 1) * ROW].rearrange("p (r w) -> p r w", w=W) for j in range(3)]
+        warm = const.tile([P, O], BF16)
+        uq_i = uq[:].bitcast(I32)
+        us_i = us[:].bitcast(I32)
 
         nc.vector.memset(warm[:], 0.0)
         nc.vector.memset(bias_row[:], 0.0)
         nc.scalar.dma_start(out=bias_row[0:1, :], in_=bias.unsqueeze(0))
-        def load_x(b):
+        for b in range(B):
             nc.sync.dma_start(
                 out=x_sb[:, b].rearrange("p t q -> p (t q)"),
                 in_=x[b].rearrange("(p t) h w -> p (t h w)", t=4),
             )
-
-        def load_w(k):
+        for k in W_ORDER:
             nc.sync.dma_start(out=w_sb[k][:], in_=Wk[k].rearrange("(n ot) c -> n (ot c)", ot=4))
-
-        for b in range(B):
-            load_x(b)
-        load_w(W_ORDER[0])
-        for k in W_ORDER[1:]:
-            load_w(k)
         make_identity(nc, ident[:])
         nc.gpsimd.memset(half[:], 0.5)
         nc.gpsimd.memset(mhalf[:], -0.5)
         nc.gpsimd.memset(ones_bf[:], 1.0)
-        nc.gpsimd.tensor_copy(
-            out=perm[:].rearrange("p (b hh w) -> p b hh w", b=B, hh=2),
-            in_=ident[:].rearrange("p (hh b w) -> p b hh w", hh=2, b=B),
-        )
         nc.scalar.activation(out=junk[:], in_=half[:], func=ACT.Ln)
         for j in range(3):
-            nc.vector.memset(us[j][:].bitcast(I32), 0)
-            for c0 in (0, (H + 1) * ROW):
-                nc.vector.memset(uq[j][:, c0:c0 + ROW].bitcast(I32), 0)
-        nc.vector.memset(uq_w[0][:, :, 0:1], 0)
-        nc.vector.memset(uq_w[2][:, :, 15:16], 0)
+            for r0 in (0, IMG - W):
+                nc.vector.memset(uq_i[:, j, :, r0:r0 + W], 0)
+        for j, w0 in ((0, 0), (2, W - 1)):
+            nc.vector.memset(uq_i[:, j, :, W:IMG - W].rearrange("p b (h w) -> p b h w", w=W)[:, :, :, w0:w0 + 1], 0)
+            nc.vector.memset(us[:, 1, j].rearrange("p b (h w) -> p b h w", w=W)[:, :, :, w0:w0 + 1], 0)
+        for i, c0 in ((0, 0), (2, HW // 4 - 4)):
+            nc.vector.memset(us_i[:, i, :, :, c0:c0 + 4].rearrange("p j b c -> p (j b) c"), 0)
 
-        n2 = [small.tile([P, 4], F32, name="n2_%d" % g) for g in range(2)]
-        nrm = [small.tile([P, 4], F32, name="nrm_%d" % g) for g in range(2)]
-        z = [small.tile([P, 4], F32, name="z_%d" % g) for g in range(2)]
-        lg = [small.tile([P, 8], F32, name="lg_%d" % g) for g in range(2)]
-        rec = [small.tile([P, 4], F32, name="rec_%d" % g) for g in range(2)]
-        dl = [small.tile([P, 4], F32, name="dl_%d" % g) for g in range(2)]
-        s = [small.tile([P, 4], F32, name="s_%d" % g) for g in range(2)]
+        n2 = small.tile([P, 8], F32)
+        nrm = small.tile([P, 8], F32)
+        z = small.tile([P, 8], F32)
+        lp = small.tile([P, 8], F32)
+        lm = small.tile([P, 8], F32)
+        rec = small.tile([P, 8], F32)
+        dl = small.tile([P, 8], F32)
+        s = small.tile([P, 8], F32)
         diag = small.tile([P, 8, P], F32)
         grams = {}
         sbc = {}
+
+        def warm_pe(n, cols=O):
+            for m in range(n):
+                pw = ps_wt.tile([P, O], F32, tag="wt", name="pw")
+                nc.tensor.matmul(out=pw[:, 0:cols], lhsT=warm[:, 0:P], rhs=warm[:, 0:cols], start=True, stop=True)
 
         def gram_pe(b):
             grams[b] = ps_acc.tile([P, 2, P], F32, tag="acc", name="gram")
@@ -113,62 +105,61 @@ def tile_pvconv2d_kernel(tc, x, Wk, bias, out):
                     nc.tensor.matmul(out=grams[b][:, hf, :], lhsT=blk, rhs=blk, start=(t == 0), stop=(t == 3))
 
         def gram_diag(b):
-            g, h2 = divmod(b, 2)
             for hf in range(2):
-                m = 2 * h2 + hf
+                m = 2 * b + hf
                 nc.vector.scalar_tensor_tensor(
-                    out=diag[:, 4 * g + m, :], in0=grams[b][:, hf, :], scalar=1e-14, in1=ident[:],
-                    op0=ALU.add, op1=ALU.mult, accum_out=n2[g][:, m:m + 1],
+                    out=diag[:, m, :], in0=grams[b][:, hf, :], scalar=1e-14, in1=ident[:],
+                    op0=ALU.add, op1=ALU.mult, accum_out=n2[:, m:m + 1],
                 )
 
-        def c_pow(g):
-            nc.gpsimd.tensor_tensor(out=nrm[g][:], in0=n2[g][:], in1=half[:, 0:4], op=ALU.pow)
+        def c_pow(m0, m1):
+            nc.gpsimd.tensor_tensor(out=nrm[:, m0:m1], in0=n2[:, m0:m1], in1=half[:, m0:m1], op=ALU.pow)
 
-        def c_z(g):
+        def c_z(m0, m1):
             nc.vector.tensor_scalar(
-                out=z[g][:], in0=nrm[g][:], scalar1=10.0 * (1.0 - 1e-6), scalar2=None, op0=ALU.min
+                out=z[:, m0:m1], in0=nrm[:, m0:m1], scalar1=10.0 * (1.0 - 1e-6), scalar2=None, op0=ALU.min
             )
-            nc.scalar.activation(out=lg[g][:, 0:4], in_=z[g][:], func=ACT.Ln, bias=1.0, scale=0.1)
-            nc.scalar.activation(out=lg[g][:, 4:8], in_=z[g][:], func=ACT.Ln, bias=1.0, scale=-0.1)
-            nc.vector.reciprocal(out=rec[g][:], in_=nrm[g][:])
+            nc.scalar.activation(out=lp[:, m0:m1], in_=z[:, m0:m1], func=ACT.Ln, bias=1.0, scale=0.1)
+            nc.scalar.activation(out=lm[:, m0:m1], in_=z[:, m0:m1], func=ACT.Ln, bias=1.0, scale=-0.1)
+            nc.vector.reciprocal(out=rec[:, m0:m1], in_=nrm[:, m0:m1])
 
-        def c_s(g):
-            nc.vector.tensor_tensor(out=dl[g][:], in0=lg[g][:, 0:4], in1=lg[g][:, 4:8], op=ALU.subtract)
+        def c_s(m0, m1):
+            nc.vector.tensor_tensor(out=dl[:, m0:m1], in0=lp[:, m0:m1], in1=lm[:, m0:m1], op=ALU.subtract)
             nc.vector.scalar_tensor_tensor(
-                out=s[g][:], in0=dl[g][:], scalar=5.0, in1=rec[g][:], op0=ALU.mult, op1=ALU.mult
+                out=s[:, m0:m1], in0=dl[:, m0:m1], scalar=5.0, in1=rec[:, m0:m1], op0=ALU.mult, op1=ALU.mult
             )
 
-        def spread(g):
-            sbc[g] = ps_acc.tile([P, 4 * P], F32, tag="acc", name="sbc")
-            for mm in range(4):
+        def spread(b):
+            sbc[b] = ps_acc.tile([P, HW], F32, tag="acc", name="sbc")
+            for hf in range(2):
+                m = 2 * b + hf
                 nc.tensor.transpose(
-                    sbc[g][:, mm * P:(mm + 1) * P], s[g][:, mm:mm + 1].to_broadcast([P, P]), ident[:]
+                    sbc[b][:, hf * P:(hf + 1) * P], s[:, m:m + 1].to_broadcast([P, P]), ident[:]
                 )
 
-        def u_mul(h0, nh, bs=(0, 1, 2, 3)):
-            for b in bs:
-                nc.vector.tensor_tensor(
-                    out=g_t[:, h0:h0 + nh, b, :, :],
-                    in0=x_sb[:, b, :, h0 * W:(h0 + nh) * W].rearrange("p t (h w) -> p h w t", h=nh),
-                    in1=sbc[b // 2][:, (b % 2) * HW + h0 * W:(b % 2) * HW + (h0 + nh) * W]
-                    .rearrange("p (h w) -> p h w", h=nh)
-                    .unsqueeze(3)
-                    .to_broadcast([P, nh, W, 4]),
-                    op=ALU.mult,
-                )
-
-        def u_shift(h0, nh, j):
-            r = slice(h0 * B, (h0 + nh) * B)
-            dst, src = (slice(1, 16), slice(0, 15)) if j == 0 else (slice(0, 15), slice(1, 16))
-            nc.vector.tensor_copy(out=uq_w[j][:, r, dst], in_=uq_w[1][:, r, src])
-            nc.vector.tensor_copy(out=us_w[j][:, r, dst], in_=us_w[1][:, r, src])
-
-        def u_quant(h0, nh):
-            nc.vector.quantize_mx(
-                out=uq[1][:, (h0 + 1) * ROW:(h0 + nh + 1) * ROW].bitcast(FP8X4),
-                scales=us[1][:, (h0 + 1) * ROW:(h0 + nh + 1) * ROW],
-                in_=line[:, h0 * ROW * 4:(h0 + nh) * ROW * 4],
+        def u_mul(b):
+            nc.vector.tensor_tensor(
+                out=g_t[:, b].rearrange("p (q t) -> p q t", t=4),
+                in0=x_sb[:, b].rearrange("p t q -> p q t"),
+                in1=sbc[b][:].unsqueeze(2).to_broadcast([P, HW, 4]),
+                op=ALU.mult,
             )
+
+        def u_quant(b):
+            nc.vector.quantize_mx(
+                out=uq[:, 1, b, W:W + HW].bitcast(FP8X4), scales=us[:, 1, 1, b, :], in_=g_t[:, b]
+            )
+
+        def u_rows(b0, b1, j):
+            nc.vector.tensor_copy(out=us_i[:, 0, j, b0:b1, 4:64], in_=us_i[:, 1, j, b0:b1, 0:60])
+            nc.vector.tensor_copy(out=us_i[:, 2, j, b0:b1, 0:60], in_=us_i[:, 1, j, b0:b1, 4:64])
+
+        def u_cols(b0, b1, j):
+            d, e = (slice(1, W), slice(0, W - 1)) if j == 0 else (slice(0, W - 1), slice(1, W))
+            cq = [uq_i[:, jj, b0:b1, W:W + HW].rearrange("p b (h w) -> p b h w", w=W) for jj in (j, 1)]
+            cs = [us[:, 1, jj, b0:b1, :].rearrange("p b (h w) -> p (b h) w", w=W) for jj in (j, 1)]
+            nc.vector.tensor_copy(out=cq[0][:, :, :, d], in_=cq[1][:, :, :, e])
+            nc.vector.tensor_copy(out=cs[0][:, :, d], in_=cs[1][:, :, e])
 
         def bias_pe():
             pb = ps_wt.tile([P, O], F32, tag="wt")
@@ -184,63 +175,70 @@ def tile_pvconv2d_kernel(tc, x, Wk, bias, out):
         wts = {}
         wgs = {}
 
-        def warm_pe(n):
-            for m in range(n):
-                pw = ps_wt.tile([P, O], F32, tag="wt", name="pw")
-                nc.tensor.matmul(out=pw[:], lhsT=warm[:, 0:P], rhs=warm[:], start=True, stop=True)
-
         wps = {}
 
-        def w_perm(k):
-            wps[k] = wp_pool.tile([P, 4, 2, P], F32, tag="wp", name="wp")
-            nc.vector.tensor_copy(
-                out=wps[k][:], in_=w_sb[k][:].bitcast(F32).rearrange("p (ot n u) -> p ot u n", ot=4, u=2)
-            )
+        def w_perm(n, eng="v"):
+            wps[n] = wp_pool.tile([P, 4, 2, P], F32, tag="wp", name="wp")
+            src = w_sb[W_ORDER[n]][:].bitcast(F32).rearrange("p (ot n u) -> p ot u n", ot=4, u=2)
+            if eng == "v":
+                nc.vector.tensor_copy(out=wps[n][:], in_=src)
+            else:
+                nc.scalar.copy(out=wps[n][:], in_=src)
 
-        def w_pe(k, hhs=(0, 1)):
+        def w_pe(n, hh):
+            k = W_ORDER[n]
             wf = w_sb[k][:].bitcast(F32)
-            for hh in hhs:
-                wt = ps_wt.tile([P, 2, 2 * P], F32, tag="wt")
-                for u in range(2):
-                    for o2 in range(2):
-                        ot = 2 * hh + o2
-                        nc.tensor.transpose(
-                            wt[:, u, o2 * P:(o2 + 1) * P],
-                            wps[k][:, ot, u, :] if k in wps else wf[:, 256 * ot + u:256 * (ot + 1):2],
-                            ident[:],
-                        )
-                wts[(k, hh)] = wt
+            wt = ps_wt.tile([P, 2, 2 * P], F32, tag="wt")
+            for u in range(2):
+                for o2 in range(2):
+                    ot = 2 * hh + o2
+                    words = wps[n][:, ot, u, :] if n in wps else wf[:, 256 * ot + u:256 * (ot + 1):2]
+                    nc.tensor.transpose(wt[:, u, o2 * P:(o2 + 1) * P], words, ident[:])
+            wts[(n, hh)] = wt
 
-        def w_out(k, hh, eng):
-            if hh == 0:
-                wgs[k] = wg_pool.tile([P, 4 * O], BF16, tag="wg", align_bytes=64, name="wg")
-            dst = wgs[k][:].bitcast(F32)[:, hh * 512:(hh + 1) * 512].rearrange("p (c u) -> p c u", u=2)
-            src = wts[(k, hh)][:].rearrange("p u c -> p c u")
+        def w_out(n, hh, eng="s"):
+            if n not in wgs:
+                wgs[n] = wg_pool.tile([P, 4 * O], BF16, tag="wg", align_bytes=64, name="wg")
+            dst = wgs[n][:].bitcast(F32)[:, hh * 512:(hh + 1) * 512].rearrange("p (c u) -> p c u", u=2)
+            src = wts[(n, hh)][:].rearrange("p u c -> p c u")
             if eng == "v":
                 nc.vector.tensor_copy(out=dst, in_=src)
             else:
                 nc.scalar.copy(out=dst, in_=src)
 
-        def w_quant(k):
-            nc.vector.quantize_mx(out=wq[k][:].bitcast(FP8X4), scales=ws[k][:], in_=wgs[k][:])
+        def w_in(n, eng0="s", eng1="s"):
+            w_pe(n, 0)
+            w_out(n, 0, eng0)
+            w_pe(n, 1)
+            w_out(n, 1, eng1)
+
+        def w_quant(*ns):
+            for n in ns:
+                k = W_ORDER[n]
+                nc.vector.quantize_mx(out=wq[k][:].bitcast(FP8X4), scales=ws[k][:], in_=wgs[n][:])
+
+        def tanh_table(n):
+            nc.scalar.activation(out=junk[:, 0:1], in_=wgs[n][:, 0:1], func=ACT.Tanh)
 
         accs = {}
         done = {}
 
-        def mx(T, ks, half=None):
-            key = T if half is None else (T, half)
-            cols = slice(0, O) if half is None else slice(half * 256, half * 256 + 256)
+        def mx(T, ns, part=None):
+            key = T if part is None else (T, part)
+            cols = slice(0, O) if part is None else slice(part * 256, part * 256 + 256)
             if key not in accs:
-                accs[key] = ps_acc.tile([P, O if half is None else 256], F32, tag="acc", name="acc")
+                accs[key] = ps_acc.tile([P, O if part is None else 256], F32, tag="acc", name="acc")
                 done[key] = 0
-            for k in ks:
+            b, hf = divmod(T, 2)
+            for n in ns:
                 done[key] += 1
+                k = W_ORDER[n]
                 i, j = divmod(k, 3)
-                c0 = (2 * T + i) * ROW
+                c0 = (8 * hf + i) * W
                 nc.tensor.matmul_mx(
                     out=accs[key][:],
-                    lhsT=uq[j][:, c0:c0 + P].bitcast(FP8X4),
-                    lhsT_scale=us[j][:, c0:c0 + P],
+                    lhsT=uq[:, j, b, c0:c0 + P].bitcast(FP8X4),
+                    lhsT_scale=us[:, i, j, b, hf * P:(hf + 1) * P],
                     rhs=wq[k][:, cols].bitcast(FP8X4),
                     rhs_scale=ws[k][:, cols],
                     start=(done[key] == 1),
@@ -285,35 +283,45 @@ def tile_pvconv2d_kernel(tc, x, Wk, bias, out):
             rs = tl[T]
             pt = ps_wt.tile([P, O], F32, tag="wt")
             for ot in range(4):
-                nc.tensor.transpose(pt[:, ot * P:(ot + 1) * P], rs[:, ot * P:(ot + 1) * P], perm[:])
+                nc.tensor.transpose(pt[:, ot * P:(ot + 1) * P], rs[:, ot * P:(ot + 1) * P], ident[:])
             tl[T] = pt
 
         def tail_c(T, eng="s"):
-            dst = o_sb[:, :, :, 32 * T:32 * T + 32]
-            src = tl[T][:].rearrange("p (ot b q) -> p b ot q", ot=4, b=B)
+            b, hf = divmod(T, 2)
+            dst = o_sb[:, b, :, hf * P:(hf + 1) * P]
+            src = tl[T][:].rearrange("p (ot q) -> p ot q", ot=4)
             if eng == "v":
                 nc.vector.tensor_copy(out=dst, in_=src)
             else:
                 nc.scalar.copy(out=dst, in_=src)
 
+        def store(T):
+            b, hf = divmod(T, 2)
+            q = slice(hf * P, (hf + 1) * P)
+            nc.sync.dma_start(out=out_v[b][:, :, q], in_=o_sb[:, b, :, q])
+
         lh = {}
 
-        def last_a(T, half):
-            cols = slice(half * 256, half * 256 + 256)
+        def last_a(T, part):
+            cols = slice(part * 256, part * 256 + 256)
             t_h = stage.tile([P, 256], F32, tag="t_h")
-            nc.vector.tensor_tensor(out=t_h[:], in0=accs[(T, half)][:], in1=bias_bc[:, cols], op=ALU.add)
+            nc.vector.tensor_tensor(out=t_h[:], in0=accs[(T, part)][:], in1=bias_bc[:, cols], op=ALU.add)
             sq_h = stage.tile([P, 256], F32, tag="sq_h")
             m2_h = tsmall.tile([P, 1], F32, tag="m2_h")
             nc.vector.scalar_tensor_tensor(
                 out=sq_h[:], in0=t_h[:], scalar=0.0, in1=t_h[:], op0=ALU.max, op1=ALU.mult, accum_out=m2_h[:]
             )
-            lh[half] = (t_h, m2_h)
+            lh[part] = (t_h, m2_h)
 
-        def last_b(T):
-            (t_a, m2_a), (t_b, m2_b) = lh[0], lh[1]
+        def last_floor():
+            m2_f = tsmall.tile([P, 1], F32, tag="m2_f")
+            nc.vector.tensor_scalar(out=m2_f[:], in0=lh[0][1][:], scalar1=1e-14, scalar2=None, op0=ALU.max)
+            lh[2] = m2_f
+
+        def last_b():
             a2 = tsmall.tile([P, 1], F32, tag="a2")
             nc.vector.tensor_scalar(
-                out=a2[:], in0=m2_b[:], scalar1=lh[2][:, 0:1], scalar2=0.01, op0=ALU.add, op1=ALU.mult
+                out=a2[:], in0=lh[1][1][:], scalar1=lh[2][:, 0:1], scalar2=0.01, op0=ALU.add, op1=ALU.mult
             )
             qv = tsmall.tile([P, 1], F32, tag="qv")
             nc.gpsimd.tensor_tensor(out=qv[:], in0=a2[:], in1=mhalf[:, 0:1], op=ALU.pow)
@@ -325,6 +333,8 @@ def tile_pvconv2d_kernel(tc, x, Wk, bias, out):
 
         def last_c(T):
             (t_a, m2_a), (t_b, m2_b), gs = lh[0], lh[1], lh[3]
+            b, hf = divmod(T, 2)
+            q = slice(hf * P, (hf + 1) * P)
             rs_a = stage.tile([P, 256], F32, tag="rs_a")
             rs_b = stage.tile([P, 256], F32, tag="rs_b")
             nc.scalar.activation(out=rs_a[:], in_=t_a[:], func=ACT.Relu, scale=gs[:, 0:1])
@@ -335,177 +345,153 @@ def tile_pvconv2d_kernel(tc, x, Wk, bias, out):
             pt_b = ps_wt.tile([P, 256], F32, tag="wt")
             for pt, rs_h in ((pt_b, rs_b), (pt_a, rs_a)):
                 for o2 in range(2):
-                    nc.tensor.transpose(pt[:, o2 * P:(o2 + 1) * P], rs_h[:, o2 * P:(o2 + 1) * P], perm[:])
-            nc.vector.tensor_copy(
-                out=o_sb[:, :, 2:4, 32 * T:32 * T + 32],
-                in_=pt_b[:].rearrange("p (ot b q) -> p b ot q", ot=2, b=B),
-            )
-            nc.scalar.copy(
-                out=o_sb[:, :, 0:2, 32 * T:32 * T + 32],
-                in_=pt_a[:].rearrange("p (ot b q) -> p b ot q", ot=2, b=B),
-            )
-
-        def last_floor():
-            m2_f = tsmall.tile([P, 1], F32, tag="m2_f")
-            nc.vector.tensor_scalar(out=m2_f[:], in0=lh[0][1][:], scalar1=1e-14, scalar2=None, op0=ALU.max)
-            lh[2] = m2_f
-
-        def tanh_table(k):
-            nc.scalar.activation(out=junk[:, 0:1], in_=wgs[k][:, 0:1], func=ACT.Tanh)
-
-        def store(q0, q1):
-            for b in range(B):
-                nc.sync.dma_start(out=out_v[b][:, :, q0:q1], in_=o_sb[:, b, :, q0:q1])
+                    nc.tensor.transpose(pt[:, o2 * P:(o2 + 1) * P], rs_h[:, o2 * P:(o2 + 1) * P], ident[:])
+            nc.vector.tensor_copy(out=o_sb[:, b, 2:4, q], in_=pt_b[:].rearrange("p (ot q) -> p ot q", ot=2))
+            nc.scalar.copy(out=o_sb[:, b, 0:2, q], in_=pt_a[:].rearrange("p (ot q) -> p ot q", ot=2))
 
         ctx.enter_context(tc.manual_schedule())
-        WO = W_ORDER
         warm_pe(3)
-        for b in range(4):
-            gram_pe(b)
-            gram_diag(b)
-            if b % 2 == 1:
-                c_pow(b // 2)
-        w_perm(WO[0])
-        warm_pe(2)
-        w_pe(WO[0])
-        c_z(0)
-        w_perm(WO[1])
-        c_s(0)
-        w_out(WO[0], 0, "s")
-        warm_pe(1)
+        gram_pe(0)
+        gram_diag(0)
+        c_pow(0, 2)
+        gram_pe(1)
+        gram_diag(1)
+        gram_pe(2)
+        gram_diag(2)
+        c_z(0, 2)
+        gram_pe(3)
+        gram_diag(3)
+        c_pow(2, 8)
+        w_pe(0, 0)
+        w_pe(0, 1)
+        w_out(0, 0, "s")
+        c_s(0, 2)
+        w_out(0, 1, "v")
+        w_pe(1, 0)
+        w_out(1, 0)
         spread(0)
-        c_z(1)
-        w_out(WO[0], 1, "s")
-        w_pe(WO[1])
-        warm_pe(1)
-        w_out(WO[1], 0, "s")
-        w_perm(WO[2])
-        u_mul(0, 4, (0,))
-        c_s(1)
+        w_pe(1, 1)
+        w_out(1, 1)
+        u_mul(0)
+        c_z(2, 8)
+        w_quant(0)
+        w_in(2)
+        u_quant(0)
+        c_s(2, 8)
+        w_perm(3)
+        u_rows(0, 1, 1)
+        w_quant(1)
         spread(1)
-        w_out(WO[1], 1, "s")
-        w_pe(WO[2])
-        warm_pe(1)
-        u_mul(0, 4, (1, 2, 3))
-        w_quant(WO[0])
-        u_quant(0, 4)
-        w_out(WO[2], 0, "s")
-        w_out(WO[2], 1, "s")
-        w_pe(WO[3], (0,))
-        warm_pe(1)
-        w_pe(WO[3], (1,))
-        warm_pe(1)
-        w_out(WO[3], 0, "s")
-        w_out(WO[3], 1, "s")
-        w_quant(WO[1])
-        mx(0, WO[0:1])
-        w_pe(WO[4], (0,))
-        warm_pe(1)
-        w_pe(WO[4], (1,))
-        w_out(WO[4], 0, "s")
-        w_out(WO[4], 1, "s")
-        mx(0, WO[1:2])
-        u_mul(4, 4)
-        w_quant(WO[2])
-        u_quant(4, 4)
-        w_pe(WO[5])
-        w_out(WO[5], 0, "s")
-        w_out(WO[5], 1, "s")
-        mx(0, WO[2:3])
-        mx(1, WO[0:3])
-        mx(2, WO[0:3])
-        u_shift(0, 8, 0)
-        w_quant(WO[3])
-        w_quant(WO[4])
-        w_pe(WO[6])
-        w_out(WO[6], 0, "s")
-        w_out(WO[6], 1, "s")
-        for T in range(3):
-            mx(T, WO[3:4])
-        u_mul(8, 8)
-        u_quant(8, 8)
-        w_pe(WO[7])
-        w_out(WO[7], 0, "s")
-        w_out(WO[7], 1, "s")
-        for T in range(3):
-            mx(T, WO[4:5])
-        w_pe(WO[8])
-        w_out(WO[8], 0, "s")
-        w_out(WO[8], 1, "s")
+        spread(2)
+        w_in(3)
+        mx(0, (0, 1))
+        mx(1, (0, 1))
+        w_perm(4)
+        u_mul(1)
+        spread(3)
+        w_in(4)
+        w_quant(2)
+        mx(0, (2,))
+        mx(1, (2,))
+        u_quant(1)
+        w_perm(5)
+        u_rows(1, 2, 1)
+        w_in(5)
+        mx(2, (0, 1, 2))
+        mx(3, (0, 1, 2))
+        u_cols(0, 2, 0)
+        w_quant(3)
+        w_perm(6)
+        u_rows(0, 2, 0)
+        w_in(6)
+        for T in range(4):
+            mx(T, (3,))
+        w_quant(4)
+        w_perm(7)
+        u_mul(2)
+        w_in(7)
+        for T in range(4):
+            mx(T, (4,))
+        w_quant(5)
+        w_perm(8)
+        u_mul(3)
+        w_in(8)
+        for T in range(4):
+            mx(T, (5,))
         pb = bias_pe()
-        tanh_table(WO[8])
+        tanh_table(8)
         bias_out(pb)
-        for T in (3, 4):
-            mx(T, WO[0:3])
-        w_quant(WO[5])
-        u_shift(8, 8, 0)
-        for T in range(3):
-            mx(T, WO[5:6])
-        u_shift(0, 8, 2)
-        for n in (6, 7, 8):
-            w_quant(WO[n])
-        for T in (3, 4):
-            mx(T, WO[3:6])
-        for T in range(3):
-            mx(T, WO[6:9])
-        u_shift(8, 8, 2)
-        for T in (3, 4):
-            mx(T, WO[6:9])
+        w_quant(6)
+        u_cols(0, 2, 2)
+        w_quant(7)
+        u_rows(0, 2, 2)
+        w_quant(8)
+        for T in range(4):
+            mx(T, (6, 7, 8))
+        u_quant(2)
+        u_quant(3)
+        u_rows(2, 4, 1)
+        u_cols(2, 4, 0)
+        u_cols(2, 4, 2)
+        u_rows(2, 4, 0)
+        u_rows(2, 4, 2)
         tail_add(0)
         tail_add(1)
         tail_sq(0)
         tail_add(2)
         tail_sq(1)
         tail_th(0)
+        mx(4, range(9))
         tail_add(3)
         tail_sq(2)
         tail_th(1)
         tail_relu(0)
-        mx(5, WO)
-        tail_add(4)
         tail_sq(3)
         tail_th(2)
         tail_relu(1)
-        mx(6, WO[0:3])
-        tail_pe(0)
-        tail_pe(1)
-        tail_add(5)
-        tail_sq(4)
+        mx(5, range(9))
         tail_th(3)
         tail_relu(2)
+        tail_pe(0)
+        tail_pe(1)
         tail_c(0)
-        mx(6, WO[3:9])
-        tail_pe(2)
-        tail_sq(5)
+        store(0)
+        tail_c(1)
+        store(1)
+        tail_add(4)
+        tail_sq(4)
         tail_th(4)
         tail_relu(3)
-        tail_c(1)
-        store(0, 64)
-        mx(7, WO, 0)
-        tail_pe(3)
-        tail_add(6)
+        tail_add(5)
+        tail_sq(5)
+        mx(6, range(9))
         tail_th(5)
         tail_relu(4)
+        tail_pe(2)
+        tail_pe(3)
         tail_c(2)
-        tail_sq(6)
-        mx(7, WO[0:4], 1)
-        tail_pe(4)
-        mx(7, WO[4:9], 1)
-        last_a(7, 0)
-        last_floor()
-        tail_relu(5)
+        store(2)
         tail_c(3)
-        store(64, 128)
-        tail_pe(5)
+        store(3)
+        tail_relu(5)
+        tail_add(6)
+        mx(7, range(9), 0)
+        tail_pe(4)
+        tail_sq(6)
         tail_th(6)
         tail_c(4)
+        store(4)
+        last_a(7, 0)
+        last_floor()
+        mx(7, range(9), 1)
         tail_relu(6)
-        last_a(7, 1)
+        tail_pe(5)
         tail_c(5)
-        store(128, 192)
+        store(5)
+        last_a(7, 1)
+        last_b()
         tail_pe(6)
-        last_b(7)
         tail_c(6, "v")
-        store(192, 224)
+        store(6)
         last_c(7)
-        store(224, 256)
+        store(7)

@@ -139,9 +139,9 @@ def tile_pvconv2d_kernel(tc, x, Wk, bias, out):
 
         def u_mul(b):
             nc.vector.tensor_tensor(
-                out=g_t[:, b].rearrange("p (q t) -> p q t", t=4),
-                in0=x_sb[:, b].rearrange("p t q -> p q t"),
-                in1=sbc[b][:].unsqueeze(2).to_broadcast([P, HW, 4]),
+                out=g_t[:, b].rearrange("p (q i t) -> p q t i", i=4, t=4),
+                in0=x_sb[:, b].rearrange("p t (q i) -> p q t i", i=4),
+                in1=sbc[b][:].rearrange("p (q i) -> p q i", i=4).unsqueeze(2).to_broadcast([P, HW // 4, 4, 4]),
                 op=ALU.mult,
             )
 

@@ -31,10 +31,10 @@ def tile_pvconv2d_kernel(tc, x, Wk, bias, out):
         t_pool = ctx.enter_context(tc.tile_pool(name="t_pool", bufs=5))
         rs_pool = ctx.enter_context(tc.tile_pool(name="rs_pool", bufs=6))
         tsmall = ctx.enter_context(tc.tile_pool(name="tsmall", bufs=8))
-        wp_pool = ctx.enter_context(tc.tile_pool(name="wp_pool", bufs=4))
         wg_pool = ctx.enter_context(tc.tile_pool(name="wg_pool", bufs=9))
         ps_wt = ctx.enter_context(tc.psum_pool(name="ps_wt", bufs=3))
-        ps_acc = ctx.enter_context(tc.psum_pool(name="ps_acc", bufs=5))
+        ps_acc = ctx.enter_context(tc.psum_pool(name="ps_acc", bufs=4))
+        ps_s = ctx.enter_context(tc.psum_pool(name="ps_s", bufs=1))
 
         x_sb = big.tile([P, B, 4, HW], BF16)
         w_sb = [big.tile([P, 4 * C], BF16, name="w_sb%d" % k) for k in range(NPOS)]
@@ -130,7 +130,7 @@ def tile_pvconv2d_kernel(tc, x, Wk, bias, out):
             )
 
         def spread(b):
-            sbc[b] = ps_acc.tile([P, HW], F32, tag="acc", name="sbc")
+            sbc[b] = ps_s.tile([P, HW], F32, tag="s", name="sbc")
             for hf in range(2):
                 m = 2 * b + hf
                 nc.tensor.transpose(
@@ -175,16 +175,6 @@ def tile_pvconv2d_kernel(tc, x, Wk, bias, out):
         wts = {}
         wgs = {}
 
-        wps = {}
-
-        def w_perm(n, eng="v"):
-            wps[n] = wp_pool.tile([P, 4, 2, P], F32, tag="wp", name="wp")
-            src = w_sb[W_ORDER[n]][:].bitcast(F32).rearrange("p (ot n u) -> p ot u n", ot=4, u=2)
-            if eng == "v":
-                nc.vector.tensor_copy(out=wps[n][:], in_=src)
-            else:
-                nc.scalar.copy(out=wps[n][:], in_=src)
-
         def w_pe(n, hh):
             k = W_ORDER[n]
             wf = w_sb[k][:].bitcast(F32)
@@ -192,8 +182,9 @@ def tile_pvconv2d_kernel(tc, x, Wk, bias, out):
             for u in range(2):
                 for o2 in range(2):
                     ot = 2 * hh + o2
-                    words = wps[n][:, ot, u, :] if n in wps else wf[:, 256 * ot + u:256 * (ot + 1):2]
-                    nc.tensor.transpose(wt[:, u, o2 * P:(o2 + 1) * P], words, ident[:])
+                    nc.tensor.transpose(
+                        wt[:, u, o2 * P:(o2 + 1) * P], wf[:, 256 * ot + u:256 * (ot + 1):2], ident[:]
+                    )
             wts[(n, hh)] = wt
 
         def w_out(n, hh, eng="s"):
@@ -378,63 +369,57 @@ def tile_pvconv2d_kernel(tc, x, Wk, bias, out):
         w_in(2)
         u_quant(0)
         c_s(2, 8)
-        w_perm(3)
         u_rows(0, 1, 1)
         w_quant(1)
-        spread(1)
-        spread(2)
         w_in(3)
+        spread(1)
         mx(0, (0, 1))
         mx(1, (0, 1))
-        w_perm(4)
         u_mul(1)
-        spread(3)
-        w_in(4)
         w_quant(2)
+        u_quant(1)
+        w_in(4)
+        spread(2)
         mx(0, (2,))
         mx(1, (2,))
-        u_quant(1)
-        w_perm(5)
         u_rows(1, 2, 1)
+        u_cols(0, 2, 0)
+        w_quant(3)
+        u_rows(0, 2, 0)
         w_in(5)
         mx(2, (0, 1, 2))
         mx(3, (0, 1, 2))
-        u_cols(0, 2, 0)
-        w_quant(3)
-        w_perm(6)
-        u_rows(0, 2, 0)
+        u_mul(2)
+        spread(3)
+        w_quant(4)
+        u_quant(2)
         w_in(6)
         for T in range(4):
             mx(T, (3,))
-        w_quant(4)
-        w_perm(7)
-        u_mul(2)
+        u_mul(3)
+        w_quant(5)
+        u_quant(3)
+        u_cols(0, 2, 2)
         w_in(7)
         for T in range(4):
             mx(T, (4,))
-        w_quant(5)
-        w_perm(8)
-        u_mul(3)
+        u_rows(0, 2, 2)
+        w_quant(6)
+        u_rows(2, 4, 1)
         w_in(8)
         for T in range(4):
             mx(T, (5,))
         pb = bias_pe()
         tanh_table(8)
         bias_out(pb)
-        w_quant(6)
-        u_cols(0, 2, 2)
-        w_quant(7)
-        u_rows(0, 2, 2)
-        w_quant(8)
-        for T in range(4):
-            mx(T, (6, 7, 8))
-        u_quant(2)
-        u_quant(3)
-        u_rows(2, 4, 1)
         u_cols(2, 4, 0)
+        w_quant(7)
         u_cols(2, 4, 2)
         u_rows(2, 4, 0)
         u_rows(2, 4, 2)
+        w_quant(8)
+        for T in range(4):
+            mx(T, (6, 7, 8))
         tail_add(0)
         tail_add(1)
         tail_sq(0)

@@ -31,6 +31,7 @@ def tile_pvconv2d_kernel(tc, x, Wk, bias, out):
         t_pool = ctx.enter_context(tc.tile_pool(name="t_pool", bufs=5))
         rs_pool = ctx.enter_context(tc.tile_pool(name="rs_pool", bufs=6))
         tsmall = ctx.enter_context(tc.tile_pool(name="tsmall", bufs=8))
+        wp_pool = ctx.enter_context(tc.tile_pool(name="wp_pool", bufs=4))
         wg_pool = ctx.enter_context(tc.tile_pool(name="wg_pool", bufs=9))
         ps_wt = ctx.enter_context(tc.psum_pool(name="ps_wt", bufs=3))
         ps_acc = ctx.enter_context(tc.psum_pool(name="ps_acc", bufs=4))
@@ -175,6 +176,16 @@ def tile_pvconv2d_kernel(tc, x, Wk, bias, out):
         wts = {}
         wgs = {}
 
+        wps = {}
+
+        def w_perm(n, eng="v"):
+            wps[n] = wp_pool.tile([P, 4, 2, P], F32, tag="wp", name="wp")
+            src = w_sb[W_ORDER[n]][:].bitcast(F32).rearrange("p (ot n u) -> p ot u n", ot=4, u=2)
+            if eng == "v":
+                nc.vector.tensor_copy(out=wps[n][:], in_=src)
+            else:
+                nc.scalar.copy(out=wps[n][:], in_=src)
+
         def w_pe(n, hh):
             k = W_ORDER[n]
             wf = w_sb[k][:].bitcast(F32)
@@ -182,9 +193,8 @@ def tile_pvconv2d_kernel(tc, x, Wk, bias, out):
             for u in range(2):
                 for o2 in range(2):
                     ot = 2 * hh + o2
-                    nc.tensor.transpose(
-                        wt[:, u, o2 * P:(o2 + 1) * P], wf[:, 256 * ot + u:256 * (ot + 1):2], ident[:]
-                    )
+                    words = wps[n][:, ot, u, :] if n in wps else wf[:, 256 * ot + u:256 * (ot + 1):2]
+                    nc.tensor.transpose(wt[:, u, o2 * P:(o2 + 1) * P], words, ident[:])
             wts[(n, hh)] = wt
 
         def w_out(n, hh, eng="s"):
@@ -318,27 +328,32 @@ def tile_pvconv2d_kernel(tc, x, Wk, bias, out):
             nc.gpsimd.tensor_tensor(out=qv[:], in0=a2[:], in1=mhalf[:, 0:1], op=ALU.pow)
             th = tsmall.tile([P, 1], F32, tag="th")
             nc.scalar.activation(out=th[:], in_=a2[:], func=ACT.Tanh, scale=qv[:, 0:1])
-            gs = tsmall.tile([P, 1], F32, tag="gs")
-            nc.gpsimd.tensor_tensor(out=gs[:], in0=th[:], in1=qv[:], op=ALU.mult)
-            lh[3] = gs
+            lh[3] = (qv, th)
+
+        def last_r(part):
+            r_h = stage.tile([P, 256], F32, tag="r_h")
+            nc.scalar.activation(out=r_h[:], in_=lh[part][0][:], func=ACT.Relu)
+            lh[4 + part] = r_h
 
         def last_c(T):
-            (t_a, m2_a), (t_b, m2_b), gs = lh[0], lh[1], lh[3]
             b, hf = divmod(T, 2)
             q = slice(hf * P, (hf + 1) * P)
-            rs_a = stage.tile([P, 256], F32, tag="rs_a")
-            rs_b = stage.tile([P, 256], F32, tag="rs_b")
-            nc.scalar.activation(out=rs_a[:], in_=t_a[:], func=ACT.Relu, scale=gs[:, 0:1])
-            nc.vector.tensor_scalar(
-                out=rs_b[:], in0=t_b[:], scalar1=gs[:, 0:1], scalar2=0.0, op0=ALU.mult, op1=ALU.max
-            )
-            pt_a = ps_wt.tile([P, 256], F32, tag="wt")
-            pt_b = ps_wt.tile([P, 256], F32, tag="wt")
-            for pt, rs_h in ((pt_b, rs_b), (pt_a, rs_a)):
+            qv, th = lh[3]
+            for part in range(2):
+                rs_h = stage.tile([P, 256], F32, tag="rs_h")
+                nc.vector.tensor_scalar(
+                    out=rs_h[:], in0=lh[4 + part][:], scalar1=qv[:, 0:1], scalar2=th[:, 0:1], op0=ALU.mult, op1=ALU.mult
+                )
+                pt_h = ps_wt.tile([P, 256], F32, tag="wt", name="pt_h")
                 for o2 in range(2):
-                    nc.tensor.transpose(pt[:, o2 * P:(o2 + 1) * P], rs_h[:, o2 * P:(o2 + 1) * P], ident[:])
-            nc.vector.tensor_copy(out=o_sb[:, b, 2:4, q], in_=pt_b[:].rearrange("p (ot q) -> p ot q", ot=2))
-            nc.scalar.copy(out=o_sb[:, b, 0:2, q], in_=pt_a[:].rearrange("p (ot q) -> p ot q", ot=2))
+                    nc.tensor.transpose(pt_h[:, o2 * P:(o2 + 1) * P], rs_h[:, o2 * P:(o2 + 1) * P], ident[:])
+                dst = o_sb[:, b, 2 * part:2 * part + 2, q]
+                src = pt_h[:].rearrange("p (ot q) -> p ot q", ot=2)
+                if part == 0:
+                    nc.scalar.copy(out=dst, in_=src)
+                else:
+                    nc.vector.tensor_copy(out=dst, in_=src)
+                nc.sync.dma_start(out=out_v[b][:, 2 * part:2 * part + 2, q], in_=dst)
 
         ctx.enter_context(tc.manual_schedule())
         warm_pe(3)
@@ -371,6 +386,7 @@ def tile_pvconv2d_kernel(tc, x, Wk, bias, out):
         c_s(2, 8)
         u_rows(0, 1, 1)
         w_quant(1)
+        w_perm(4, "s")
         w_in(3)
         spread(1)
         mx(0, (0, 1))
@@ -386,6 +402,7 @@ def tile_pvconv2d_kernel(tc, x, Wk, bias, out):
         u_cols(0, 2, 0)
         w_quant(3)
         u_rows(0, 2, 0)
+        w_perm(6, "s")
         w_in(5)
         mx(2, (0, 1, 2))
         mx(3, (0, 1, 2))
@@ -400,6 +417,7 @@ def tile_pvconv2d_kernel(tc, x, Wk, bias, out):
         w_quant(5)
         u_quant(3)
         u_cols(0, 2, 2)
+        w_perm(8, "s")
         w_in(7)
         for T in range(4):
             mx(T, (4,))
@@ -467,6 +485,7 @@ def tile_pvconv2d_kernel(tc, x, Wk, bias, out):
         tail_c(4)
         store(4)
         last_a(7, 0)
+        last_r(0)
         last_floor()
         mx(7, range(9), 1)
         tail_relu(6)
@@ -474,9 +493,9 @@ def tile_pvconv2d_kernel(tc, x, Wk, bias, out):
         tail_c(5)
         store(5)
         last_a(7, 1)
+        last_r(1)
         last_b()
         tail_pe(6)
         tail_c(6, "v")
         store(6)
         last_c(7)
-        store(7)

@@ -16,6 +16,7 @@ P = 128
 B, C, O, H, W = 4, 512, 512, 16, 16
 HW = H * W
 IMG = (H + 2) * W
+IMG_PITCH = 320
 NPOS = 9
 W_ORDER = (4, 1, 7, 3, 0, 6, 5, 2, 8)
 FLOPS = 2 * B * HW * C * NPOS * O
@@ -39,11 +40,11 @@ def tile_pvconv2d_kernel(tc, x, Wk, bias, out):
 
         x_sb = big.tile([P, B, 4, HW], BF16)
         w_sb = [big.tile([P, 4 * C], BF16, name="w_sb%d" % k) for k in range(NPOS)]
-        wq = [big.tile([P, O], U32, name="wq%d" % k, align_bytes=64) for k in range(NPOS)]
-        ws = [big.tile([P, O], U8, name="ws%d" % k, align_bytes=64) for k in range(NPOS)]
-        g_t = big.tile([P, B, HW * 4], BF16, align_bytes=64)
-        uq = big.tile([P, 3, B, IMG], U32, align_bytes=64)
-        us = big.tile([P, 3, 3, B, HW], U8, align_bytes=64)
+        wq = [big.tile([P, O], U32, name="wq%d" % k, align_bytes=256) for k in range(NPOS)]
+        ws = [big.tile([P, O], U8, name="ws%d" % k, align_bytes=256) for k in range(NPOS)]
+        g_t = big.tile([P, B, HW * 4], BF16, align_bytes=256)
+        uq = big.tile([P, 3, B, IMG_PITCH], U32, align_bytes=256)
+        us = big.tile([P, 3, 3, B, HW], U8, align_bytes=256)
         o_sb = big.tile([P, B, 4, HW], F32)
         out_v = out.rearrange("b (n ot) h w -> b n ot (h w)", ot=4)
         ident = const.tile([P, P], F32)
@@ -199,7 +200,7 @@ def tile_pvconv2d_kernel(tc, x, Wk, bias, out):
 
         def w_out(n, hh, eng="s"):
             if n not in wgs:
-                wgs[n] = wg_pool.tile([P, 4 * O], BF16, tag="wg", align_bytes=64, name="wg")
+                wgs[n] = wg_pool.tile([P, 4 * O], BF16, tag="wg", align_bytes=256, name="wg")
             dst = wgs[n][:].bitcast(F32)[:, hh * 512:(hh + 1) * 512].rearrange("p (c u) -> p c u", u=2)
             src = wts[(n, hh)][:].rearrange("p u c -> p c u")
             if eng == "v":

@@ -50,17 +50,13 @@ def tile_pvconv2d_kernel(tc, x, Wk, bias, out):
         ident = const.tile([P, P], F32)
         half = const.tile([P, 8], F32)
         mhalf = const.tile([P, 8], F32)
-        ones_bf = const.tile([P, P], BF16)
-        bias_row = const.tile([P, O], BF16)
-        bias_bc = const.tile([P, O], F32)
+        bias_bc = const.tile([P, O], BF16)
         junk = const.tile([P, 8], F32)
         warm = const.tile([P, O], BF16)
         uq_i = uq[:].bitcast(I32)
         us_i = us[:].bitcast(I32)
 
         nc.vector.memset(warm[:], 0.0)
-        nc.vector.memset(bias_row[:], 0.0)
-        nc.scalar.dma_start(out=bias_row[0:1, :], in_=bias.unsqueeze(0))
         for b in range(B):
             nc.sync.dma_start(
                 out=x_sb[:, b].rearrange("p t q -> p (t q)"),
@@ -68,10 +64,10 @@ def tile_pvconv2d_kernel(tc, x, Wk, bias, out):
             )
         for k in W_ORDER:
             nc.sync.dma_start(out=w_sb[k][:], in_=Wk[k].rearrange("(n ot) c -> n (ot c)", ot=4))
+        nc.sync.dma_start(out=bias_bc[:], in_=bias.partition_broadcast(P))
         make_identity(nc, ident[:])
         nc.gpsimd.memset(half[:], 0.5)
         nc.gpsimd.memset(mhalf[:], -0.5)
-        nc.gpsimd.memset(ones_bf[:], 1.0)
         nc.scalar.activation(out=junk[:], in_=half[:], func=ACT.Ln)
         for j in range(3):
             for r0 in (0, IMG - W):
@@ -163,16 +159,7 @@ def tile_pvconv2d_kernel(tc, x, Wk, bias, out):
             nc.vector.tensor_copy(out=cq[0][:, :, :, d], in_=cq[1][:, :, :, e])
             nc.vector.tensor_copy(out=cs[0][:, :, d], in_=cs[1][:, :, e])
 
-        def bias_pe():
-            pb = ps_wt.tile([P, O], F32, tag="wt")
-            nc.tensor.matmul(out=pb[:], lhsT=ones_bf[:], rhs=bias_row[:], start=True, stop=True)
-            return pb
-
-        def bias_out(pb):
-            nc.scalar.copy(
-                out=bias_bc[:].rearrange("p (ot n) -> p ot n", ot=4),
-                in_=pb[:].rearrange("p (n ot) -> p ot n", ot=4),
-            )
+        bias_v = bias_bc[:].rearrange("p (n ot) -> p ot n", ot=4)
 
         wts = {}
         wgs = {}
@@ -251,7 +238,12 @@ def tile_pvconv2d_kernel(tc, x, Wk, bias, out):
 
         def tail_add(T):
             t_sb = t_pool.tile([P, O], F32, tag="t")
-            nc.vector.tensor_tensor(out=t_sb[:], in0=accs[T][:], in1=bias_bc[:], op=ALU.add)
+            nc.vector.tensor_tensor(
+                out=t_sb[:].rearrange("p (ot n) -> p ot n", ot=4),
+                in0=accs[T][:].rearrange("p (ot n) -> p ot n", ot=4),
+                in1=bias_v,
+                op=ALU.add,
+            )
             tl[T] = t_sb
 
         def tail_sq(T):
@@ -307,7 +299,12 @@ def tile_pvconv2d_kernel(tc, x, Wk, bias, out):
         def last_a(T, part):
             cols = slice(part * 256, part * 256 + 256)
             t_h = stage.tile([P, 256], F32, tag="t_h")
-            nc.vector.tensor_tensor(out=t_h[:], in0=accs[(T, part)][:], in1=bias_bc[:, cols], op=ALU.add)
+            nc.vector.tensor_tensor(
+                out=t_h[:].rearrange("p (ot n) -> p ot n", n=P),
+                in0=accs[(T, part)][:].rearrange("p (ot n) -> p ot n", n=P),
+                in1=bias_v[:, cols.start // P:cols.stop // P],
+                op=ALU.add,
+            )
             sq_h = stage.tile([P, 256], F32, tag="sq_h")
             m2_h = tsmall.tile([P, 1], F32, tag="m2_h")
             nc.vector.scalar_tensor_tensor(
@@ -320,13 +317,17 @@ def tile_pvconv2d_kernel(tc, x, Wk, bias, out):
             nc.vector.tensor_scalar(out=m2_f[:], in0=lh[0][1][:], scalar1=1e-14, scalar2=None, op0=ALU.max)
             lh[2] = m2_f
 
-        def last_b():
+        def last_b_v():
             a2 = tsmall.tile([P, 1], F32, tag="a2")
             nc.vector.tensor_scalar(
                 out=a2[:], in0=lh[1][1][:], scalar1=lh[2][:, 0:1], scalar2=0.01, op0=ALU.add, op1=ALU.mult
             )
             qv = tsmall.tile([P, 1], F32, tag="qv")
             nc.gpsimd.tensor_tensor(out=qv[:], in0=a2[:], in1=mhalf[:, 0:1], op=ALU.pow)
+            lh[3] = (a2, qv)
+
+        def last_b_s():
+            a2, qv = lh[3]
             th = tsmall.tile([P, 1], F32, tag="th")
             nc.scalar.activation(out=th[:], in_=a2[:], func=ACT.Tanh, scale=qv[:, 0:1])
             lh[3] = (qv, th)
@@ -395,6 +396,7 @@ def tile_pvconv2d_kernel(tc, x, Wk, bias, out):
         u_mul(1)
         w_quant(2)
         u_quant(1)
+        w_perm(5, "s")
         w_in(4)
         spread(2)
         mx(0, (2,))
@@ -428,9 +430,7 @@ def tile_pvconv2d_kernel(tc, x, Wk, bias, out):
         w_in(8)
         for T in range(4):
             mx(T, (5,))
-        pb = bias_pe()
         tanh_table(8)
-        bias_out(pb)
         u_cols(2, 4, 0)
         w_quant(7)
         u_cols(2, 4, 2)
@@ -438,7 +438,9 @@ def tile_pvconv2d_kernel(tc, x, Wk, bias, out):
         u_rows(2, 4, 2)
         w_quant(8)
         for T in range(4):
-            mx(T, (6, 7, 8))
+            mx(T, (6,))
+        for T in range(4):
+            mx(T, (7, 8))
         tail_add(0)
         tail_add(1)
         tail_sq(0)
@@ -480,23 +482,24 @@ def tile_pvconv2d_kernel(tc, x, Wk, bias, out):
         tail_relu(5)
         tail_add(6)
         mx(7, range(9), 0)
-        tail_pe(4)
         tail_sq(6)
         tail_th(6)
-        tail_c(4)
-        store(4)
         last_a(7, 0)
         last_r(0)
         last_floor()
         mx(7, range(9), 1)
-        tail_relu(6)
+        tail_pe(4)
         tail_pe(5)
-        tail_c(5)
-        store(5)
+        tail_relu(6)
+        tail_c(4)
+        store(4)
         last_a(7, 1)
         last_r(1)
-        last_b()
+        last_b_v()
         tail_pe(6)
+        tail_c(5, "v")
+        store(5)
+        last_b_s()
         tail_c(6, "v")
         store(6)
         last_c(7)

@@ -413,6 +413,7 @@ def tile_pvconv2d_kernel(tc, x, Wk, bias, out):
         spread(3)
         w_quant(4)
         u_quant(2)
+        w_perm(7, "s")
         w_in(6)
         for T in range(4):
             mx(T, (3,))
@@ -431,12 +432,12 @@ def tile_pvconv2d_kernel(tc, x, Wk, bias, out):
         for T in range(4):
             mx(T, (5,))
         tanh_table(8)
-        u_cols(2, 4, 0)
         w_quant(7)
+        u_cols(2, 4, 0)
+        w_quant(8)
         u_cols(2, 4, 2)
         u_rows(2, 4, 0)
         u_rows(2, 4, 2)
-        w_quant(8)
         for T in range(4):
             mx(T, (6,))
         for T in range(4):

from contextlib import ExitStack

import concourse.mybir as mybir
from concourse.masks import make_identity

F32 = mybir.dt.float32
BF16 = mybir.dt.bfloat16
U32 = mybir.dt.uint32
U8 = mybir.dt.uint8
I32 = mybir.dt.int32
FP8X4 = mybir.dt.float8_e4m3fn_x4
ALU = mybir.AluOpType
ACT = mybir.ActivationFunctionType

P = 128
B, C, O, H, W = 4, 512, 512, 16, 16
HW = H * W
IMG = (H + 2) * W
IMG_PITCH = 320
NPOS = 9
W_ORDER = (4, 1, 7, 3, 0, 6, 5, 2, 8)
FLOPS = 2 * B * HW * C * NPOS * O


def tile_pvconv2d_kernel(tc, x, Wk, bias, out):
    nc = tc.nc
    with ExitStack() as ctx:
        const = ctx.enter_context(tc.tile_pool(name="const", bufs=1))
        big = ctx.enter_context(tc.tile_pool(name="big", bufs=1))
        stage = ctx.enter_context(tc.tile_pool(name="stage", bufs=3))
        small = ctx.enter_context(tc.tile_pool(name="small", bufs=1))
        t_pool = ctx.enter_context(tc.tile_pool(name="t_pool", bufs=5))
        rs_pool = ctx.enter_context(tc.tile_pool(name="rs_pool", bufs=6))
        tsmall = ctx.enter_context(tc.tile_pool(name="tsmall", bufs=8))
        wp_pool = ctx.enter_context(tc.tile_pool(name="wp_pool", bufs=4))
        wg_pool = ctx.enter_context(tc.tile_pool(name="wg_pool", bufs=9))
        ps_wt = ctx.enter_context(tc.psum_pool(name="ps_wt", bufs=3))
        ps_acc = ctx.enter_context(tc.psum_pool(name="ps_acc", bufs=4))
        ps_s = ctx.enter_context(tc.psum_pool(name="ps_s", bufs=1))

        x_sb = big.tile([P, B, 4, HW], BF16)
        w_sb = [big.tile([P, 4 * C], BF16, name="w_sb%d" % k) for k in range(NPOS)]
        wq = [big.tile([P, O], U32, name="wq%d" % k, align_bytes=256) for k in range(NPOS)]
        ws = [big.tile([P, O], U8, name="ws%d" % k, align_bytes=256) for k in range(NPOS)]
        g_t = big.tile([P, B, HW * 4], BF16, align_bytes=256)
        uq = big.tile([P, 3, B, IMG_PITCH], U32, align_bytes=256)
        us = big.tile([P, 3, 3, B, HW], U8, align_bytes=256)
        o_sb = big.tile([P, B, 4, HW], F32)
        out_v = out.rearrange("b (n ot) h w -> b n ot (h w)", ot=4)
        ident = const.tile([P, P], F32)
        half = const.tile([P, 8], F32)
        mhalf = const.tile([P, 8], F32)
        bias_bc = const.tile([P, O], BF16)
        junk = const.tile([P, 8], F32)
        warm = const.tile([P, O], BF16)
        uq_i = uq[:].bitcast(I32)
        us_i = us[:].bitcast(I32)

        nc.vector.memset(warm[:], 0.0)
        for b in range(B):
            nc.sync.dma_start(
                out=x_sb[:, b].rearrange("p t q -> p (t q)"),
                in_=x[b].rearrange("(p t) h w -> p (t h w)", t=4),
            )
        for k in W_ORDER:
            nc.sync.dma_start(out=w_sb[k][:], in_=Wk[k].rearrange("(n ot) c -> n (ot c)", ot=4))
        nc.sync.dma_start(out=bias_bc[:], in_=bias.partition_broadcast(P))
        make_identity(nc, ident[:])
        nc.gpsimd.memset(half[:], 0.5)
        nc.gpsimd.memset(mhalf[:], -0.5)
        nc.scalar.activation(out=junk[:], in_=half[:], func=ACT.Ln)
        for j in range(3):
            for r0 in (0, IMG - W):
                nc.vector.memset(uq_i[:, j, :, r0:r0 + W], 0)
        for j, w0 in ((0, 0), (2, W - 1)):
            nc.vector.memset(uq_i[:, j, :, W:IMG - W].rearrange("p b (h w) -> p b h w", w=W)[:, :, :, w0:w0 + 1], 0)
            nc.vector.memset(us[:, 1, j].rearrange("p b (h w) -> p b h w", w=W)[:, :, :, w0:w0 + 1], 0)
        for i, c0 in ((0, 0), (2, HW // 4 - 4)):
            nc.vector.memset(us_i[:, i, :, :, c0:c0 + 4].rearrange("p j b c -> p (j b) c"), 0)

        n2 = small.tile([P, 8], F32)
        nrm = small.tile([P, 8], F32)
        z = small.tile([P, 8], F32)
        lp = small.tile([P, 8], F32)
        lm = small.tile([P, 8], F32)
        rec = small.tile([P, 8], F32)
        dl = small.tile([P, 8], F32)
        s = small.tile([P, 8], F32)
        diag = small.tile([P, 8, P], F32)
        grams = {}
        sbc = {}

        def warm_pe(n, cols=O):
            for m in range(n):
                pw = ps_wt.tile([P, O], F32, tag="wt", name="pw")
                nc.tensor.matmul(out=pw[:, 0:cols], lhsT=warm[:, 0:P], rhs=warm[:, 0:cols], start=True, stop=True)

        def gram_pe(b):
            grams[b] = ps_acc.tile([P, 2, P], F32, tag="acc", name="gram")
            for hf in range(2):
                for t in range(4):
                    blk = x_sb[:, b, t, hf * P:(hf + 1) * P]
                    nc.tensor.matmul(out=grams[b][:, hf, :], lhsT=blk, rhs=blk, start=(t == 0), stop=(t == 3))

        def gram_diag(b):
            for hf in range(2):
                m = 2 * b + hf
                nc.vector.scalar_tensor_tensor(
                    out=diag[:, m, :], in0=grams[b][:, hf, :], scalar=1e-14, in1=ident[:],
                    op0=ALU.add, op1=ALU.mult, accum_out=n2[:, m:m + 1],
                )

        def c_pow(m0, m1):
            nc.gpsimd.tensor_tensor(out=nrm[:, m0:m1], in0=n2[:, m0:m1], in1=half[:, m0:m1], op=ALU.pow)

        def c_z(m0, m1):
            nc.vector.tensor_scalar(
                out=z[:, m0:m1], in0=nrm[:, m0:m1], scalar1=10.0 * (1.0 - 1e-6), scalar2=None, op0=ALU.min
            )
            nc.scalar.activation(out=lp[:, m0:m1], in_=z[:, m0:m1], func=ACT.Ln, bias=1.0, scale=0.1)
            nc.scalar.activation(out=lm[:, m0:m1], in_=z[:, m0:m1], func=ACT.Ln, bias=1.0, scale=-0.1)
            nc.vector.reciprocal(out=rec[:, m0:m1], in_=nrm[:, m0:m1])

        def c_s(m0, m1):
            nc.vector.tensor_tensor(out=dl[:, m0:m1], in0=lp[:, m0:m1], in1=lm[:, m0:m1], op=ALU.subtract)
            nc.vector.scalar_tensor_tensor(
                out=s[:, m0:m1], in0=dl[:, m0:m1], scalar=5.0, in1=rec[:, m0:m1], op0=ALU.mult, op1=ALU.mult
            )

        def spread(b):
            sbc[b] = ps_s.tile([P, HW], F32, tag="s", name="sbc")
            for hf in range(2):
                m = 2 * b + hf
                nc.tensor.transpose(
                    sbc[b][:, hf * P:(hf + 1) * P], s[:, m:m + 1].to_broadcast([P, P]), ident[:]
                )

        def u_mul(b):
            nc.vector.tensor_tensor(
                out=g_t[:, b].rearrange("p (q i t) -> p q t i", i=4, t=4),
                in0=x_sb[:, b].rearrange("p t (q i) -> p q t i", i=4),
                in1=sbc[b][:].rearrange("p (q i) -> p q i", i=4).unsqueeze(2).to_broadcast([P, HW // 4, 4, 4]),
                op=ALU.mult,
            )

        def u_quant(b):
            nc.vector.quantize_mx(
                out=uq[:, 1, b, W:W + HW].bitcast(FP8X4), scales=us[:, 1, 1, b, :], in_=g_t[:, b]
            )

        def u_rows(b0, b1, j):
            nc.vector.tensor_copy(out=us_i[:, 0, j, b0:b1, 4:64], in_=us_i[:, 1, j, b0:b1, 0:60])
            nc.vector.tensor_copy(out=us_i[:, 2, j, b0:b1, 0:60], in_=us_i[:, 1, j, b0:b1, 4:64])

        def u_cols(b0, b1, j):
            d, e = (slice(1, W), slice(0, W - 1)) if j == 0 else (slice(0, W - 1), slice(1, W))
            cq = [uq_i[:, jj, b0:b1, W:W + HW].rearrange("p b (h w) -> p b h w", w=W) for jj in (j, 1)]
            cs = [us[:, 1, jj, b0:b1, :].rearrange("p b (h w) -> p (b h) w", w=W) for jj in (j, 1)]
            nc.vector.tensor_copy(out=cq[0][:, :, :, d], in_=cq[1][:, :, :, e])
            nc.vector.tensor_copy(out=cs[0][:, :, d], in_=cs[1][:, :, e])

        bias_v = bias_bc[:].rearrange("p (n ot) -> p ot n", ot=4)

        wts = {}
        wgs = {}

        wps = {}

        def w_perm(n, eng="v"):
            wps[n] = wp_pool.tile([P, 4, 2, P], F32, tag="wp", name="wp")
            src = w_sb[W_ORDER[n]][:].bitcast(F32).rearrange("p (ot n u) -> p ot u n", ot=4, u=2)
            if eng == "v":
                nc.vector.tensor_copy(out=wps[n][:], in_=src)
            else:
                nc.scalar.copy(out=wps[n][:], in_=src)

        def w_pe(n, hh):
            k = W_ORDER[n]
            wf = w_sb[k][:].bitcast(F32)
            wt = ps_wt.tile([P, 2, 2 * P], F32, tag="wt")
            for u in range(2):
                for o2 in range(2):
                    ot = 2 * hh + o2
                    words = wps[n][:, ot, u, :] if n in wps else wf[:, 256 * ot + u:256 * (ot + 1):2]
                    nc.tensor.transpose(wt[:, u, o2 * P:(o2 + 1) * P], words, ident[:])
            wts[(n, hh)] = wt

        def w_out(n, hh, eng="s"):
            if n not in wgs:
                wgs[n] = wg_pool.tile([P, 4 * O], BF16, tag="wg", align_bytes=256, name="wg")
            dst = wgs[n][:].bitcast(F32)[:, hh * 512:(hh + 1) * 512].rearrange("p (c u) -> p c u", u=2)
            src = wts[(n, hh)][:].rearrange("p u c -> p c u")
            if eng == "v":
                nc.vector.tensor_copy(out=dst, in_=src)
            else:
                nc.scalar.copy(out=dst, in_=src)

        def w_in(n, eng0="s", eng1="s"):
            w_pe(n, 0)
            w_out(n, 0, eng0)
            w_pe(n, 1)
            w_out(n, 1, eng1)

        def w_quant(*ns):
            for n in ns:
                k = W_ORDER[n]
                nc.vector.quantize_mx(out=wq[k][:].bitcast(FP8X4), scales=ws[k][:], in_=wgs[n][:])

        def tanh_table(n):
            nc.scalar.activation(out=junk[:, 0:1], in_=wgs[n][:, 0:1], func=ACT.Tanh)

        accs = {}
        done = {}

        def mx(T, ns, part=None):
            key = T if part is None else (T, part)
            cols = slice(0, O) if part is None else slice(part * 256, part * 256 + 256)
            if key not in accs:
                accs[key] = ps_acc.tile([P, O if part is None else 256], F32, tag="acc", name="acc")
                done[key] = 0
            b, hf = divmod(T, 2)
            for n in ns:
                done[key] += 1
                k = W_ORDER[n]
                i, j = divmod(k, 3)
                c0 = (8 * hf + i) * W
                nc.tensor.matmul_mx(
                    out=accs[key][:],
                    lhsT=uq[:, j, b, c0:c0 + P].bitcast(FP8X4),
                    lhsT_scale=us[:, i, j, b, hf * P:(hf + 1) * P],
                    rhs=wq[k][:, cols].bitcast(FP8X4),
                    rhs_scale=ws[k][:, cols],
                    start=(done[key] == 1),
                    stop=(done[key] == NPOS),
                )

        tl = {}

        def tail_add(T):
            t_sb = t_pool.tile([P, O], F32, tag="t")
            nc.vector.tensor_tensor(
                out=t_sb[:].rearrange("p (ot n) -> p ot n", ot=4),
                in0=accs[T][:].rearrange("p (ot n) -> p ot n", ot=4),
                in1=bias_v,
                op=ALU.add,
            )
            tl[T] = t_sb

        def tail_sq(T):
            t_sb = tl[T]
            sq = stage.tile([P, O], F32, tag="sq")
            m2 = tsmall.tile([P, 1], F32, tag="m2")
            nc.vector.scalar_tensor_tensor(
                out=sq[:], in0=t_sb[:], scalar=0.0, in1=t_sb[:], op0=ALU.max, op1=ALU.mult, accum_out=m2[:]
            )
            a2 = tsmall.tile([P, 1], F32, tag="a2")
            nc.gpsimd.tensor_scalar(out=a2[:], in0=m2[:], scalar1=1e-14, scalar2=0.01, op0=ALU.max, op1=ALU.mult)
            qv = tsmall.tile([P, 1], F32, tag="qv")
            nc.gpsimd.tensor_tensor(out=qv[:], in0=a2[:], in1=mhalf[:, 0:1], op=ALU.pow)
            tl[T] = (t_sb, a2, qv)

        def tail_th(T):
            t_sb, a2, qv = tl[T]
            th = tsmall.tile([P, 1], F32, tag="th")
            nc.scalar.activation(out=th[:], in_=a2[:], func=ACT.Tanh, scale=qv[:, 0:1])
            gs = tsmall.tile([P, 1], F32, tag="gs")
            nc.gpsimd.tensor_tensor(out=gs[:], in0=th[:], in1=qv[:], op=ALU.mult)
            tl[T] = (t_sb, gs)

        def tail_relu(T):
            t_sb, gs = tl[T]
            rs = rs_pool.tile([P, O], F32, tag="rs")
            nc.scalar.activation(out=rs[:], in_=t_sb[:], func=ACT.Relu, scale=gs[:, 0:1])
            tl[T] = rs

        def tail_pe(T):
            rs = tl[T]
            pt = ps_wt.tile([P, O], F32, tag="wt")
            for ot in range(4):
                nc.tensor.transpose(pt[:, ot * P:(ot + 1) * P], rs[:, ot * P:(ot + 1) * P], ident[:])
            tl[T] = pt

        def tail_c(T, eng="s"):
            b, hf = divmod(T, 2)
            dst = o_sb[:, b, :, hf * P:(hf + 1) * P]
            src = tl[T][:].rearrange("p (ot q) -> p ot q", ot=4)
            if eng == "v":
                nc.vector.tensor_copy(out=dst, in_=src)
            else:
                nc.scalar.copy(out=dst, in_=src)

        def store(T):
            b, hf = divmod(T, 2)
            q = slice(hf * P, (hf + 1) * P)
            nc.sync.dma_start(out=out_v[b][:, :, q], in_=o_sb[:, b, :, q])

        lh = {}

        def last_a(T, part):
            cols = slice(part * 256, part * 256 + 256)
            t_h = stage.tile([P, 256], F32, tag="t_h")
            nc.vector.tensor_tensor(
                out=t_h[:].rearrange("p (ot n) -> p ot n", n=P),
                in0=accs[(T, part)][:].rearrange("p (ot n) -> p ot n", n=P),
                in1=bias_v[:, cols.start // P:cols.stop // P],
                op=ALU.add,
            )
            sq_h = stage.tile([P, 256], F32, tag="sq_h")
            m2_h = tsmall.tile([P, 1], F32, tag="m2_h")
            nc.vector.scalar_tensor_tensor(
                out=sq_h[:], in0=t_h[:], scalar=0.0, in1=t_h[:], op0=ALU.max, op1=ALU.mult, accum_out=m2_h[:]
            )
            lh[part] = (t_h, m2_h)

        def last_floor():
            m2_f = tsmall.tile([P, 1], F32, tag="m2_f")
            nc.vector.tensor_scalar(out=m2_f[:], in0=lh[0][1][:], scalar1=1e-14, scalar2=None, op0=ALU.max)
            lh[2] = m2_f

        def last_b_v():
            a2 = tsmall.tile([P, 1], F32, tag="a2")
            nc.vector.tensor_scalar(
                out=a2[:], in0=lh[1][1][:], scalar1=lh[2][:, 0:1], scalar2=0.01, op0=ALU.add, op1=ALU.mult
            )
            qv = tsmall.tile([P, 1], F32, tag="qv")
            nc.gpsimd.tensor_tensor(out=qv[:], in0=a2[:], in1=mhalf[:, 0:1], op=ALU.pow)
            lh[3] = (a2, qv)

        def last_b_s():
            a2, qv = lh[3]
            th = tsmall.tile([P, 1], F32, tag="th")
            nc.scalar.activation(out=th[:], in_=a2[:], func=ACT.Tanh, scale=qv[:, 0:1])
            lh[3] = (qv, th)

        def last_r(part):
            r_h = stage.tile([P, 256], F32, tag="r_h")
            nc.scalar.activation(out=r_h[:], in_=lh[part][0][:], func=ACT.Relu)
            lh[4 + part] = r_h

        def last_c(T):
            b, hf = divmod(T, 2)
            q = slice(hf * P, (hf + 1) * P)
            qv, th = lh[3]
            for part in range(2):
                rs_h = stage.tile([P, 256], F32, tag="rs_h")
                nc.vector.tensor_scalar(
                    out=rs_h[:], in0=lh[4 + part][:], scalar1=qv[:, 0:1], scalar2=th[:, 0:1], op0=ALU.mult, op1=ALU.mult
                )
                pt_h = ps_wt.tile([P, 256], F32, tag="wt", name="pt_h")
                for o2 in range(2):
                    nc.tensor.transpose(pt_h[:, o2 * P:(o2 + 1) * P], rs_h[:, o2 * P:(o2 + 1) * P], ident[:])
                dst = o_sb[:, b, 2 * part:2 * part + 2, q]
                src = pt_h[:].rearrange("p (ot q) -> p ot q", ot=2)
                if part == 0:
                    nc.scalar.copy(out=dst, in_=src)
                else:
                    nc.vector.tensor_copy(out=dst, in_=src)
                nc.sync.dma_start(out=out_v[b][:, 2 * part:2 * part + 2, q], in_=dst)

        ctx.enter_context(tc.manual_schedule())
        warm_pe(3)
        gram_pe(0)
        gram_diag(0)
        c_pow(0, 2)
        gram_pe(1)
        gram_diag(1)
        gram_pe(2)
        gram_diag(2)
        c_z(0, 2)
        gram_pe(3)
        gram_diag(3)
        c_pow(2, 8)
        w_pe(0, 0)
        w_pe(0, 1)
        w_out(0, 0, "s")
        c_s(0, 2)
        w_out(0, 1, "v")
        w_pe(1, 0)
        w_out(1, 0)
        spread(0)
        w_pe(1, 1)
        w_out(1, 1)
        u_mul(0)
        c_z(2, 8)
        w_quant(0)
        w_in(2)
        u_quant(0)
        c_s(2, 8)
        u_rows(0, 1, 1)
        w_quant(1)
        w_perm(4, "s")
        w_in(3)
        spread(1)
        mx(0, (0, 1))
        mx(1, (0, 1))
        u_mul(1)
        w_quant(2)
        u_quant(1)
        w_perm(5, "s")
        w_in(4)
        spread(2)
        mx(0, (2,))
        mx(1, (2,))
        u_rows(1, 2, 1)
        u_cols(0, 2, 0)
        w_quant(3)
        u_rows(0, 2, 0)
        w_perm(6, "s")
        w_in(5)
        mx(2, (0, 1, 2))
        mx(3, (0, 1, 2))
        u_mul(2)
        spread(3)
        w_quant(4)
        u_quant(2)
        w_perm(7, "s")
        w_in(6)
        for T in range(4):
            mx(T, (3,))
        u_mul(3)
        w_quant(5)
        u_quant(3)
        u_cols(0, 2, 2)
        w_perm(8, "s")
        w_in(7)
        for T in range(4):
            mx(T, (4,))
        u_rows(0, 2, 2)
        w_quant(6)
        u_rows(2, 4, 1)
        w_in(8)
        for T in range(4):
            mx(T, (5,))
        tanh_table(8)
        w_quant(7)
        u_cols(2, 4, 0)
        w_quant(8)
        u_cols(2, 4, 2)
        u_rows(2, 4, 0)
        u_rows(2, 4, 2)
        for T in range(4):
            mx(T, (6,))
        for T in range(4):
            mx(T, (7, 8))
        tail_add(0)
        tail_add(1)
        tail_sq(0)
        tail_add(2)
        tail_sq(1)
        tail_th(0)
        mx(4, range(9))
        tail_add(3)
        tail_sq(2)
        tail_th(1)
        tail_relu(0)
        tail_sq(3)
        tail_th(2)
        tail_relu(1)
        mx(5, range(9))
        tail_th(3)
        tail_relu(2)
        tail_pe(0)
        tail_pe(1)
        tail_c(0)
        store(0)
        tail_c(1)
        store(1)
        tail_add(4)
        tail_sq(4)
        tail_th(4)
        tail_relu(3)
        tail_add(5)
        tail_sq(5)
        mx(6, range(9))
        tail_th(5)
        tail_relu(4)
        tail_pe(2)
        tail_pe(3)
        tail_c(2)
        store(2)
        tail_c(3)
        store(3)
        tail_relu(5)
        tail_add(6)
        mx(7, range(9), 0)
        tail_sq(6)
        tail_th(6)
        last_a(7, 0)
        last_r(0)
        last_floor()
        mx(7, range(9), 1)
        tail_pe(4)
        tail_pe(5)
        tail_relu(6)
        tail_c(4)
        store(4)
        last_a(7, 1)
        last_r(1)
        last_b_v()
        tail_pe(6)
        tail_c(5, "v")
        store(5)
        last_b_s()
        tail_c(6, "v")
        store(6)
        last_c(7)
